import numpy as np
import ml_dtypes

BF16 = ml_dtypes.bfloat16


def bf(x):
    return np.asarray(x, np.float32).astype(BF16)


def f32(x):
    return np.asarray(x, np.float32)


def f64(x):
    return np.asarray(x).astype(np.float64)


def striped(idx):
    return np.tile(idx.reshape(-1, 16).T, (8, 1))


B, L, H, S, N, Q = 4, 512, 512, 4096, 2048, 128
TEMP = 0.2
EPS = 1e-20


def silu(a):
    return a / (1.0 + np.exp(-a))


def sigmoid(a):
    return 1.0 / (1.0 + np.exp(-a))


def setup_inputs():
    uni = np.random.uniform(size=(L, L))
    return {
        "item_emb": f32(0.8 * np.random.standard_normal((H, S))),
        "pos_emb": f32(0.6 * np.random.standard_normal((H, L))),
        "wz": bf(np.random.standard_normal((H, H)) / np.sqrt(H)),
        "wv": bf(np.random.standard_normal((H, H)) / np.sqrt(H)),
        "wq": bf(np.random.standard_normal((H, H)) / np.sqrt(H)),
        "wk": bf(np.random.standard_normal((H, H)) / np.sqrt(H)),
        "gamma_q": f32(3.0 * np.random.standard_normal((H, 1))),
        "beta_q": f32(0.3 * np.random.standard_normal((H, 1))),
        "gamma_k": f32(3.0 * np.random.standard_normal((H, 1))),
        "beta_k": f32(0.3 * np.random.standard_normal((H, 1))),
        "sparse_w": f32(np.random.uniform(0.2, 0.8, (L, L))),
        "gumbel": f32(-np.log(-np.log(uni + EPS) + EPS)),
        "valid": f32(np.concatenate([np.ones((Q, B)), np.random.uniform(size=(L - Q, B)) < 0.8])),
        "offs": striped(np.random.permutation(np.tile(np.arange(S), 2))[:N]),
    }


def reference(item_emb, pos_emb, wz, wv, wq, wk, gamma_q, beta_q, gamma_k, beta_k, sparse_w, gumbel, valid, offs):
    idx = offs[:16].T.reshape(-1)
    x = f64(item_emb)[:, idx] + np.tile(f64(pos_emb), (1, B))
    z = silu(f64(wz).T @ x)
    v = silu(f64(wv).T @ x)
    q = (f64(wq).T @ z) * f64(gamma_q) + f64(beta_q)
    k = (f64(wk).T @ z) * f64(gamma_k) + f64(beta_k)
    smask = sigmoid((np.log(f64(sparse_w) / (1.0 - f64(sparse_w))) + f64(gumbel)) / TEMP)
    pos = np.arange(L)
    before = f64(pos[:, None] < pos[None, :])
    same = f64(pos[:, None] == pos[None, :])
    res = np.zeros((H, N))
    for b in range(B):
        sl = slice(b * L, (b + 1) * L)
        keep = same + before * f64(valid)[:, b:b + 1]
        a = k[:, sl].T @ q[:, sl]
        p = np.square(np.maximum(smask * keep * a, 0.0)) / (L * H)
        res[:, sl] = v[:, sl] @ p
    return res

@@ -1,0 +1,188 @@
+import concourse.mybir as mybir
+
+F32 = mybir.dt.float32
+BF16 = mybir.dt.bfloat16
+U16 = mybir.dt.uint16
+I32 = mybir.dt.int32
+ALU = mybir.AluOpType
+ACT = mybir.ActivationFunctionType
+
+P = 128
+B, L, H, S = 4, 512, 512, 4096
+N = B * L
+HB = H // P
+LB = L // P
+TEMP = 0.2
+
+FLOPS = 4 * 2 * H * H * N + 2 * 2 * H * B * (L * (L + 1) // 2)
+
+
+def tile_denoisedsasrec_b_kernel(
+    tc, item_emb, pos_emb, wz, wv, wq, wk, gamma_q, beta_q, gamma_k, beta_k, sparse_w, gumbel, valid, offs, out
+):
+    nc = tc.nc
+    with (
+        tc.tile_pool(name="held", bufs=1) as held,
+        tc.tile_pool(name="summed", bufs=4) as summed,
+        tc.tile_pool(name="inputs", bufs=B) as inputs,
+        tc.tile_pool(name="sequence", bufs=2) as sequence,
+        tc.tile_pool(name="maskwork", bufs=2) as maskwork,
+        tc.tile_pool(name="staging", bufs=4) as staging,
+        tc.psum_pool(name="psum", bufs=8) as psum,
+    ):
+        offsets = held.tile([P, N // 16], U16, name="offsets")
+        nc.sync.dma_start(offsets[:], offs)
+        table = [held.tile([P, S], F32, name=f"table{c}") for c in range(HB)]
+        pos = [held.tile([P, L], F32, name=f"pos{c}") for c in range(HB)]
+        for c in range(HB):
+            nc.sync.dma_start(table[c][:], item_emb[c * P : (c + 1) * P, :])
+            nc.scalar.dma_start(pos[c][:], pos_emb[c * P : (c + 1) * P, :])
+
+        def load_weight(queue, weight, name):
+            tile = held.tile([P, HB, H], BF16, name=name)
+            queue.dma_start(tile[:], weight.rearrange("(c p) e -> p c e", p=P))
+            return tile
+
+        wz_sb = load_weight(nc.scalar, wz, "wz_sb")
+        wv_sb = load_weight(nc.scalar, wv, "wv_sb")
+        wq_sb = load_weight(nc.sync, wq, "wq_sb")
+        wk_sb = load_weight(nc.sync, wk, "wk_sb")
+
+        def load_column(vector, name):
+            tile = held.tile([P, HB], F32, name=name)
+            with nc.allow_non_contiguous_dma(reason="512 single floats, one to a partition and block"):
+                nc.scalar.dma_start(tile[:], vector.rearrange("(d p) o -> p (d o)", p=P))
+            return tile
+
+        gamma_q_sb = load_column(gamma_q, "gamma_q_sb")
+        beta_q_sb = load_column(beta_q, "beta_q_sb")
+        gamma_k_sb = load_column(gamma_k, "gamma_k_sb")
+        beta_k_sb = load_column(beta_k, "beta_k_sb")
+        valid_sb = held.tile([P, LB, B], F32, name="valid_sb")
+        nc.scalar.dma_start(valid_sb[:], valid.rearrange("(i p) b -> p i b", p=P))
+
+        x = [inputs.tile([P, HB, L], BF16, name="x") for b in range(B)]
+        for c in range(HB):
+            for b in range(B):
+                x_f32 = summed.tile([P, L], F32, name="x_f32")
+                picked = table[c][:].indirect(offsets[:, b * (L // 16) : (b + 1) * (L // 16)])
+                nc.vector.tensor_tensor(x_f32[:], picked, pos[c][:], ALU.add)
+                nc.scalar.copy(x[b][:, c, :], x_f32[:])
+
+        above = [held.tile([P, L], F32, name=f"above{i}") for i in range(LB)]
+        diagonal = [held.tile([P, L], F32, name=f"diagonal{i}") for i in range(LB)]
+        distance = held.tile([P, L], I32, name="distance")
+        is_above = held.tile([P, L], F32, name="is_above")
+        is_diagonal = held.tile([P, L], F32, name="is_diagonal")
+        nc.gpsimd.iota(distance[:], pattern=[[1, L]], base=0, channel_multiplier=-1)
+        nc.vector.tensor_scalar(is_above[:], distance[:], 0.0, None, ALU.is_gt)
+        nc.vector.tensor_scalar(is_diagonal[:], distance[:], 0.0, None, ALU.is_equal)
+
+        def build_shared_mask():
+            for i in range(LB):
+                rows = slice(i * P, (i + 1) * P)
+                cols = slice(i * P, L)
+                width = L - i * P
+                w_sb = maskwork.tile([P, L], F32, name="w_sb")
+                g_sb = maskwork.tile([P, L], F32, name="g_sb")
+                nc.sync.dma_start(w_sb[:, cols], sparse_w[rows, cols])
+                nc.sync.dma_start(g_sb[:, cols], gumbel[rows, cols])
+                ln_w = maskwork.tile([P, L], F32, name="ln_w")
+                ln_rest = maskwork.tile([P, L], F32, name="ln_rest")
+                nc.scalar.activation(ln_w[:, cols], w_sb[:, cols], ACT.Ln)
+                nc.scalar.activation(ln_rest[:, cols], w_sb[:, cols], ACT.Ln, bias=1.0, scale=-1.0)
+                logit = maskwork.tile([P, L], F32, name="logit")
+                noisy = maskwork.tile([P, L], F32, name="noisy")
+                nc.gpsimd.tensor_sub(logit[:, cols], ln_w[:, cols], ln_rest[:, cols])
+                nc.gpsimd.tensor_add(noisy[:, cols], logit[:, cols], g_sb[:, cols])
+                smask = maskwork.tile([P, L], F32, name="smask")
+                nc.scalar.activation(smask[:, cols], noisy[:, cols], ACT.Sigmoid, scale=1.0 / TEMP)
+                nc.gpsimd.tensor_mul(above[i][:, cols], smask[:, cols], is_above[:, 0:width])
+                nc.gpsimd.tensor_mul(diagonal[i][:, cols], smask[:, cols], is_diagonal[:, 0:width])
+
+        z, vT, q, k, mask, p = {}, {}, {}, {}, {}, {}
+
+        def project_x(b):
+            z_b = sequence.tile([P, HB, L], BF16, name="z_b")
+            for e in range(HB):
+                acc = psum.tile([P, L], F32, name="acc")
+                for c in range(HB):
+                    nc.tensor.matmul(
+                        acc[:], wz_sb[:, c, e * P : (e + 1) * P], x[b][:, c, :], start=(c == 0), stop=(c == HB - 1)
+                    )
+                nc.scalar.activation(z_b[:, e, :], acc[:], ACT.Silu)
+            vT_b = sequence.tile([P, LB, H], BF16, name="vT_b")
+            for i in range(LB):
+                acc = psum.tile([P, H], F32, name="acc")
+                for c in range(HB):
+                    nc.tensor.matmul(
+                        acc[:], x[b][:, c, i * P : (i + 1) * P], wv_sb[:, c, :], start=(c == 0), stop=(c == HB - 1)
+                    )
+                nc.scalar.activation(vT_b[:, i, :], acc[:], ACT.Silu)
+            z[b], vT[b] = z_b, vT_b
+
+        def project_z(b):
+            q_b = sequence.tile([P, HB, L], BF16, name="q_b")
+            k_b = sequence.tile([P, HB, L], BF16, name="k_b")
+            for d in range(HB):
+                for weight, gamma, beta, result in (
+                    (wq_sb, gamma_q_sb, beta_q_sb, q_b),
+                    (wk_sb, gamma_k_sb, beta_k_sb, k_b),
+                ):
+                    acc = psum.tile([P, L], F32, name="acc")
+                    for e in range(HB):
+                        nc.tensor.matmul(
+                            acc[:], weight[:, e, d * P : (d + 1) * P], z[b][:, e, :], start=(e == 0), stop=(e == HB - 1)
+                        )
+                    nc.vector.tensor_scalar(
+                        result[:, d, :], acc[:], gamma[:, d : d + 1], beta[:, d : d + 1], ALU.mult, ALU.add
+                    )
+            q[b], k[b] = q_b, k_b
+
+        def build_mask(b):
+            mask_b = sequence.tile([P, LB, L], F32, name="mask_b")
+            for i in range(LB):
+                cols = slice(i * P, L)
+                nc.vector.scalar_tensor_tensor(
+                    mask_b[:, i, cols], above[i][:, cols], valid_sb[:, i, b : b + 1], diagonal[i][:, cols], ALU.mult, ALU.add
+                )
+            mask[b] = mask_b
+
+        def scores(b):
+            p_b = sequence.tile([P, LB, L], BF16, name="p_b")
+            for i in range(LB):
+                cols = slice(i * P, L)
+                acc = psum.tile([P, L], F32, name="acc")
+                for d in range(HB):
+                    nc.tensor.matmul(
+                        acc[:, cols], k[b][:, d, i * P : (i + 1) * P], q[b][:, d, cols], start=(d == 0), stop=(d == HB - 1)
+                    )
+                kept = staging.tile([P, L], F32, name="kept")
+                nc.vector.scalar_tensor_tensor(kept[:, cols], acc[:, cols], 0.0, mask[b][:, i, cols], ALU.max, ALU.mult)
+                nc.scalar.activation(p_b[:, i, cols], kept[:, cols], ACT.Square, scale=(L * H) ** -0.5)
+            p[b] = p_b
+
+        def mix(b):
+            res = [psum.tile([P, L], F32, name="acc") for e in range(HB)]
+            for i in range(LB):
+                cols = slice(i * P, L)
+                for e in range(HB):
+                    nc.tensor.matmul(
+                        res[e][:, cols], vT[b][:, i, e * P : (e + 1) * P], p[b][:, i, cols], start=(i == 0), stop=(i == LB - 1)
+                    )
+            for e in range(HB):
+                res_sb = staging.tile([P, L], F32, name="res_sb")
+                nc.scalar.copy(res_sb[:], res[e][:])
+                nc.sync.dma_start(out[e * P : (e + 1) * P, b * L : (b + 1) * L], res_sb[:])
+
+        project_x(0)
+        build_shared_mask()
+        project_z(0)
+        for b in range(B):
+            build_mask(b)
+            if b + 1 < B:
+                project_x(b + 1)
+            scores(b)
+            if b + 1 < B:
+                project_z(b + 1)
+            mix(b)

@@ -30,23 +30,25 @@ def tile_denoisedsasrec_b_kernel(
         tc.tile_pool(name="staging", bufs=4) as staging,
         tc.psum_pool(name="psum", bufs=8) as psum,
     ):
-        offsets = held.tile([P, N // 16], U16, name="offsets")
-        nc.sync.dma_start(offsets[:], offs)
-        table = [held.tile([P, S], F32, name=f"table{c}") for c in range(HB)]
-        pos = [held.tile([P, L], F32, name=f"pos{c}") for c in range(HB)]
-        for c in range(HB):
-            nc.sync.dma_start(table[c][:], item_emb[c * P : (c + 1) * P, :])
-            nc.scalar.dma_start(pos[c][:], pos_emb[c * P : (c + 1) * P, :])
-
         def load_weight(queue, weight, name):
             tile = held.tile([P, HB, H], BF16, name=name)
             queue.dma_start(tile[:], weight.rearrange("(c p) e -> p c e", p=P))
             return tile
 
-        wz_sb = load_weight(nc.scalar, wz, "wz_sb")
-        wv_sb = load_weight(nc.scalar, wv, "wv_sb")
+        offsets = held.tile([P, N // 16], U16, name="offsets")
+        nc.sync.dma_start(offsets[:], offs)
+        table = [held.tile([P, S], F32, name=f"table{c}") for c in range(HB)]
+        for c in range(HB):
+            nc.sync.dma_start(table[c][:], item_emb[c * P : (c + 1) * P, :])
         wq_sb = load_weight(nc.sync, wq, "wq_sb")
         wk_sb = load_weight(nc.sync, wk, "wk_sb")
+
+        pos = [held.tile([P, L], F32, name=f"pos{c}") for c in range(HB)]
+        nc.scalar.dma_start(pos[0][:], pos_emb[0:P, :])
+        wz_sb = load_weight(nc.scalar, wz, "wz_sb")
+        wv_sb = load_weight(nc.scalar, wv, "wv_sb")
+        for c in range(1, HB):
+            nc.scalar.dma_start(pos[c][:], pos_emb[c * P : (c + 1) * P, :])
 
         def load_column(vector, name):
             tile = held.tile([P, HB], F32, name=name)
@@ -102,22 +104,40 @@ def tile_denoisedsasrec_b_kernel(
 
         z, vT, q, k, mask, p = {}, {}, {}, {}, {}, {}
 
+        def add_to_z(acc, b, e, c):
+            nc.tensor.matmul(acc[:], wz_sb[:, c, e * P : (e + 1) * P], x[b][:, c, :], start=(c == 0), stop=(c == HB - 1))
+
+        def add_to_vT(acc, b, i, c):
+            nc.tensor.matmul(acc[:], x[b][:, c, i * P : (i + 1) * P], wv_sb[:, c, :], start=(c == 0), stop=(c == HB - 1))
+
+        def project_first_x():
+            z_acc = [psum.tile([P, L], F32, name="acc") for e in range(HB)]
+            vT_acc = [psum.tile([P, H], F32, name="acc") for i in range(LB)]
+            for c in range(HB):
+                for e in range(HB):
+                    add_to_z(z_acc[e], 0, e, c)
+                for i in range(LB):
+                    add_to_vT(vT_acc[i], 0, i, c)
+            z_b = sequence.tile([P, HB, L], BF16, name="z_b")
+            vT_b = sequence.tile([P, LB, H], BF16, name="vT_b")
+            for e in range(HB):
+                nc.scalar.activation(z_b[:, e, :], z_acc[e][:], ACT.Silu)
+            for i in range(LB):
+                nc.scalar.activation(vT_b[:, i, :], vT_acc[i][:], ACT.Silu)
+            z[0], vT[0] = z_b, vT_b
+
         def project_x(b):
             z_b = sequence.tile([P, HB, L], BF16, name="z_b")
             for e in range(HB):
                 acc = psum.tile([P, L], F32, name="acc")
                 for c in range(HB):
-                    nc.tensor.matmul(
-                        acc[:], wz_sb[:, c, e * P : (e + 1) * P], x[b][:, c, :], start=(c == 0), stop=(c == HB - 1)
-                    )
+                    add_to_z(acc, b, e, c)
                 nc.scalar.activation(z_b[:, e, :], acc[:], ACT.Silu)
             vT_b = sequence.tile([P, LB, H], BF16, name="vT_b")
             for i in range(LB):
                 acc = psum.tile([P, H], F32, name="acc")
                 for c in range(HB):
-                    nc.tensor.matmul(
-                        acc[:], x[b][:, c, i * P : (i + 1) * P], wv_sb[:, c, :], start=(c == 0), stop=(c == HB - 1)
-                    )
+                    add_to_vT(acc, b, i, c)
                 nc.scalar.activation(vT_b[:, i, :], acc[:], ACT.Silu)
             z[b], vT[b] = z_b, vT_b
 
@@ -175,7 +195,7 @@ def tile_denoisedsasrec_b_kernel(
                 nc.scalar.copy(res_sb[:], res[e][:])
                 nc.sync.dma_start(out[e * P : (e + 1) * P, b * L : (b + 1) * L], res_sb[:])
 
-        project_x(0)
+        project_first_x()
         build_shared_mask()
         project_z(0)
         for b in range(B):

@@ -14,6 +14,15 @@ HB = H // P
 LB = L // P
 TEMP = 0.2
 
+WIDTH = [L - i * P for i in range(LB)]
+START = [sum(WIDTH[:i]) for i in range(LB)]
+PACKED = sum(WIDTH)
+
+
+def block(packed_tile, i):
+    return packed_tile[:, START[i] : START[i] + WIDTH[i]]
+
+
 FLOPS = 4 * 2 * H * H * N + 2 * 2 * H * B * (L * (L + 1) // 2)
 
 
@@ -26,34 +35,37 @@ def tile_denoisedsasrec_b_kernel(
         tc.tile_pool(name="summed", bufs=4) as summed,
         tc.tile_pool(name="inputs", bufs=B) as inputs,
         tc.tile_pool(name="sequence", bufs=2) as sequence,
-        tc.tile_pool(name="maskwork", bufs=2) as maskwork,
+        tc.tile_pool(name="values", bufs=3) as values,
+        tc.tile_pool(name="maskwork", bufs=4) as maskwork,
         tc.tile_pool(name="staging", bufs=4) as staging,
         tc.psum_pool(name="psum", bufs=8) as psum,
     ):
-        def load_weight(queue, weight, name):
+        def load_weight(weight, name):
             tile = held.tile([P, HB, H], BF16, name=name)
-            queue.dma_start(tile[:], weight.rearrange("(c p) e -> p c e", p=P))
+            nc.sync.dma_start(tile[:], weight.rearrange("(c p) e -> p c e", p=P))
             return tile
 
         offsets = held.tile([P, N // 16], U16, name="offsets")
         nc.sync.dma_start(offsets[:], offs)
         table = [held.tile([P, S], F32, name=f"table{c}") for c in range(HB)]
-        for c in range(HB):
-            nc.sync.dma_start(table[c][:], item_emb[c * P : (c + 1) * P, :])
-        wq_sb = load_weight(nc.sync, wq, "wq_sb")
-        wk_sb = load_weight(nc.sync, wk, "wk_sb")
-
         pos = [held.tile([P, L], F32, name=f"pos{c}") for c in range(HB)]
-        nc.scalar.dma_start(pos[0][:], pos_emb[0:P, :])
-        wz_sb = load_weight(nc.scalar, wz, "wz_sb")
-        wv_sb = load_weight(nc.scalar, wv, "wv_sb")
+
+        def load_table_block(c):
+            nc.sync.dma_start(pos[c][:], pos_emb[c * P : (c + 1) * P, :])
+            nc.sync.dma_start(table[c][:], item_emb[c * P : (c + 1) * P, :])
+
+        load_table_block(0)
+        wz_sb = load_weight(wz, "wz_sb")
+        wv_sb = load_weight(wv, "wv_sb")
         for c in range(1, HB):
-            nc.scalar.dma_start(pos[c][:], pos_emb[c * P : (c + 1) * P, :])
+            load_table_block(c)
+        wq_sb = load_weight(wq, "wq_sb")
+        wk_sb = load_weight(wk, "wk_sb")
 
         def load_column(vector, name):
             tile = held.tile([P, HB], F32, name=name)
             with nc.allow_non_contiguous_dma(reason="512 single floats, one to a partition and block"):
-                nc.scalar.dma_start(tile[:], vector.rearrange("(d p) o -> p (d o)", p=P))
+                nc.gpsimd.dma_start(tile[:], vector.rearrange("(d p) o -> p (d o)", p=P))
             return tile
 
         gamma_q_sb = load_column(gamma_q, "gamma_q_sb")
@@ -61,7 +73,7 @@ def tile_denoisedsasrec_b_kernel(
         gamma_k_sb = load_column(gamma_k, "gamma_k_sb")
         beta_k_sb = load_column(beta_k, "beta_k_sb")
         valid_sb = held.tile([P, LB, B], F32, name="valid_sb")
-        nc.scalar.dma_start(valid_sb[:], valid.rearrange("(i p) b -> p i b", p=P))
+        nc.gpsimd.dma_start(valid_sb[:], valid.rearrange("(i p) b -> p i b", p=P))
 
         x = [inputs.tile([P, HB, L], BF16, name="x") for b in range(B)]
         for c in range(HB):
@@ -71,36 +83,38 @@ def tile_denoisedsasrec_b_kernel(
                 nc.vector.tensor_tensor(x_f32[:], picked, pos[c][:], ALU.add)
                 nc.scalar.copy(x[b][:, c, :], x_f32[:])
 
-        above = [held.tile([P, L], F32, name=f"above{i}") for i in range(LB)]
-        diagonal = [held.tile([P, L], F32, name=f"diagonal{i}") for i in range(LB)]
-        distance = held.tile([P, L], I32, name="distance")
-        is_above = held.tile([P, L], F32, name="is_above")
-        is_diagonal = held.tile([P, L], F32, name="is_diagonal")
-        nc.gpsimd.iota(distance[:], pattern=[[1, L]], base=0, channel_multiplier=-1)
+        distance = held.tile([P, PACKED], I32, name="distance")
+        is_above = held.tile([P, PACKED], F32, name="is_above")
+        is_diagonal = held.tile([P, PACKED], F32, name="is_diagonal")
+        for i in range(LB):
+            nc.gpsimd.iota(block(distance, i), pattern=[[1, WIDTH[i]]], base=0, channel_multiplier=-1)
         nc.vector.tensor_scalar(is_above[:], distance[:], 0.0, None, ALU.is_gt)
         nc.vector.tensor_scalar(is_diagonal[:], distance[:], 0.0, None, ALU.is_equal)
+        above = held.tile([P, PACKED], F32, name="above")
+        diagonal = held.tile([P, PACKED], F32, name="diagonal")
 
         def build_shared_mask():
+            def step(name):
+                return maskwork.tile([P, PACKED], F32, name=name, tag="step")
+
+            w_sb = step("w_sb")
+            g_sb = step("g_sb")
             for i in range(LB):
                 rows = slice(i * P, (i + 1) * P)
-                cols = slice(i * P, L)
-                width = L - i * P
-                w_sb = maskwork.tile([P, L], F32, name="w_sb")
-                g_sb = maskwork.tile([P, L], F32, name="g_sb")
-                nc.sync.dma_start(w_sb[:, cols], sparse_w[rows, cols])
-                nc.sync.dma_start(g_sb[:, cols], gumbel[rows, cols])
-                ln_w = maskwork.tile([P, L], F32, name="ln_w")
-                ln_rest = maskwork.tile([P, L], F32, name="ln_rest")
-                nc.scalar.activation(ln_w[:, cols], w_sb[:, cols], ACT.Ln)
-                nc.scalar.activation(ln_rest[:, cols], w_sb[:, cols], ACT.Ln, bias=1.0, scale=-1.0)
-                logit = maskwork.tile([P, L], F32, name="logit")
-                noisy = maskwork.tile([P, L], F32, name="noisy")
-                nc.gpsimd.tensor_sub(logit[:, cols], ln_w[:, cols], ln_rest[:, cols])
-                nc.gpsimd.tensor_add(noisy[:, cols], logit[:, cols], g_sb[:, cols])
-                smask = maskwork.tile([P, L], F32, name="smask")
-                nc.scalar.activation(smask[:, cols], noisy[:, cols], ACT.Sigmoid, scale=1.0 / TEMP)
-                nc.gpsimd.tensor_mul(above[i][:, cols], smask[:, cols], is_above[:, 0:width])
-                nc.gpsimd.tensor_mul(diagonal[i][:, cols], smask[:, cols], is_diagonal[:, 0:width])
+                nc.sync.dma_start(block(w_sb, i), sparse_w[rows, i * P : L])
+                nc.sync.dma_start(block(g_sb, i), gumbel[rows, i * P : L])
+            ln_w = step("ln_w")
+            nc.scalar.activation(ln_w[:], w_sb[:], ACT.Ln)
+            ln_rest = step("ln_rest")
+            nc.scalar.activation(ln_rest[:], w_sb[:], ACT.Ln, bias=1.0, scale=-1.0)
+            noisy = step("noisy")
+            nc.vector.tensor_add(noisy[:], ln_w[:], g_sb[:])
+            logit = step("logit")
+            nc.vector.tensor_sub(logit[:], noisy[:], ln_rest[:])
+            smask = step("smask")
+            nc.scalar.activation(smask[:], logit[:], ACT.Sigmoid, scale=1.0 / TEMP)
+            nc.vector.tensor_mul(above[:], smask[:], is_above[:])
+            nc.vector.tensor_mul(diagonal[:], smask[:], is_diagonal[:])
 
         z, vT, q, k, mask, p = {}, {}, {}, {}, {}, {}
 
@@ -119,7 +133,7 @@ def tile_denoisedsasrec_b_kernel(
                 for i in range(LB):
                     add_to_vT(vT_acc[i], 0, i, c)
             z_b = sequence.tile([P, HB, L], BF16, name="z_b")
-            vT_b = sequence.tile([P, LB, H], BF16, name="vT_b")
+            vT_b = values.tile([P, LB, H], BF16, name="vT_b")
             for e in range(HB):
                 nc.scalar.activation(z_b[:, e, :], z_acc[e][:], ACT.Silu)
             for i in range(LB):
@@ -133,7 +147,7 @@ def tile_denoisedsasrec_b_kernel(
                 for c in range(HB):
                     add_to_z(acc, b, e, c)
                 nc.scalar.activation(z_b[:, e, :], acc[:], ACT.Silu)
-            vT_b = sequence.tile([P, LB, H], BF16, name="vT_b")
+            vT_b = values.tile([P, LB, H], BF16, name="vT_b")
             for i in range(LB):
                 acc = psum.tile([P, H], F32, name="acc")
                 for c in range(HB):
@@ -160,11 +174,10 @@ def tile_denoisedsasrec_b_kernel(
             q[b], k[b] = q_b, k_b
 
         def build_mask(b):
-            mask_b = sequence.tile([P, LB, L], F32, name="mask_b")
+            mask_b = sequence.tile([P, PACKED], F32, name="mask_b")
             for i in range(LB):
-                cols = slice(i * P, L)
                 nc.vector.scalar_tensor_tensor(
-                    mask_b[:, i, cols], above[i][:, cols], valid_sb[:, i, b : b + 1], diagonal[i][:, cols], ALU.mult, ALU.add
+                    block(mask_b, i), block(above, i), valid_sb[:, i, b : b + 1], block(diagonal, i), ALU.mult, ALU.add
                 )
             mask[b] = mask_b
 
@@ -178,31 +191,35 @@ def tile_denoisedsasrec_b_kernel(
                         acc[:, cols], k[b][:, d, i * P : (i + 1) * P], q[b][:, d, cols], start=(d == 0), stop=(d == HB - 1)
                     )
                 kept = staging.tile([P, L], F32, name="kept")
-                nc.vector.scalar_tensor_tensor(kept[:, cols], acc[:, cols], 0.0, mask[b][:, i, cols], ALU.max, ALU.mult)
+                nc.vector.scalar_tensor_tensor(kept[:, cols], acc[:, cols], 0.0, block(mask[b], i), ALU.max, ALU.mult)
                 nc.scalar.activation(p_b[:, i, cols], kept[:, cols], ACT.Square, scale=(L * H) ** -0.5)
             p[b] = p_b
 
         def mix(b):
-            res = [psum.tile([P, L], F32, name="acc") for e in range(HB)]
-            for i in range(LB):
-                cols = slice(i * P, L)
-                for e in range(HB):
-                    nc.tensor.matmul(
-                        res[e][:, cols], vT[b][:, i, e * P : (e + 1) * P], p[b][:, i, cols], start=(i == 0), stop=(i == LB - 1)
-                    )
             for e in range(HB):
+                acc = psum.tile([P, L], F32, name="acc")
+                for i in range(LB):
+                    cols = slice(i * P, L)
+                    nc.tensor.matmul(
+                        acc[:, cols], vT[b][:, i, e * P : (e + 1) * P], p[b][:, i, cols], start=(i == 0), stop=(i == LB - 1)
+                    )
                 res_sb = staging.tile([P, L], F32, name="res_sb")
-                nc.scalar.copy(res_sb[:], res[e][:])
+                nc.scalar.copy(res_sb[:], acc[:])
                 nc.sync.dma_start(out[e * P : (e + 1) * P, b * L : (b + 1) * L], res_sb[:])
 
         project_first_x()
         build_shared_mask()
         project_z(0)
+        project_x(1)
+        project_z(1)
+        build_mask(0)
+        scores(0)
         for b in range(B):
-            build_mask(b)
+            if b + 2 < B:
+                project_x(b + 2)
             if b + 1 < B:
-                project_x(b + 1)
-            scores(b)
-            if b + 1 < B:
-                project_z(b + 1)
+                build_mask(b + 1)
+                scores(b + 1)
+            if b + 2 < B:
+                project_z(b + 2)
             mix(b)

@@ -35,7 +35,7 @@ def tile_denoisedsasrec_b_kernel(
         tc.tile_pool(name="summed", bufs=4) as summed,
         tc.tile_pool(name="inputs", bufs=B) as inputs,
         tc.tile_pool(name="sequence", bufs=2) as sequence,
-        tc.tile_pool(name="values", bufs=3) as values,
+        tc.tile_pool(name="values", bufs=B) as values,
         tc.tile_pool(name="maskwork", bufs=4) as maskwork,
         tc.tile_pool(name="staging", bufs=4) as staging,
         tc.psum_pool(name="psum", bufs=8) as psum,
@@ -56,9 +56,9 @@ def tile_denoisedsasrec_b_kernel(
 
         load_table_block(0)
         wz_sb = load_weight(wz, "wz_sb")
-        wv_sb = load_weight(wv, "wv_sb")
         for c in range(1, HB):
             load_table_block(c)
+        wv_sb = load_weight(wv, "wv_sb")
         wq_sb = load_weight(wq, "wq_sb")
         wk_sb = load_weight(wk, "wk_sb")
 
@@ -124,38 +124,38 @@ def tile_denoisedsasrec_b_kernel(
         def add_to_vT(acc, b, i, c):
             nc.tensor.matmul(acc[:], x[b][:, c, i * P : (i + 1) * P], wv_sb[:, c, :], start=(c == 0), stop=(c == HB - 1))
 
-        def project_first_x():
-            z_acc = [psum.tile([P, L], F32, name="acc") for e in range(HB)]
-            vT_acc = [psum.tile([P, H], F32, name="acc") for i in range(LB)]
+        def make_first_z():
+            first = range(2)
+            z_acc = [[psum.tile([P, L], F32, name="acc") for e in range(HB)] for b in first]
             for c in range(HB):
+                for b in first:
+                    for e in range(HB):
+                        add_to_z(z_acc[b][e], b, e, c)
+            for b in first:
+                z_b = sequence.tile([P, HB, L], BF16, name="z_b")
                 for e in range(HB):
-                    add_to_z(z_acc[e], 0, e, c)
-                for i in range(LB):
-                    add_to_vT(vT_acc[i], 0, i, c)
-            z_b = sequence.tile([P, HB, L], BF16, name="z_b")
-            vT_b = values.tile([P, LB, H], BF16, name="vT_b")
-            for e in range(HB):
-                nc.scalar.activation(z_b[:, e, :], z_acc[e][:], ACT.Silu)
-            for i in range(LB):
-                nc.scalar.activation(vT_b[:, i, :], vT_acc[i][:], ACT.Silu)
-            z[0], vT[0] = z_b, vT_b
+                    nc.scalar.activation(z_b[:, e, :], z_acc[b][e][:], ACT.Silu)
+                z[b] = z_b
 
-        def project_x(b):
+        def make_z(b):
             z_b = sequence.tile([P, HB, L], BF16, name="z_b")
             for e in range(HB):
                 acc = psum.tile([P, L], F32, name="acc")
                 for c in range(HB):
                     add_to_z(acc, b, e, c)
                 nc.scalar.activation(z_b[:, e, :], acc[:], ACT.Silu)
+            z[b] = z_b
+
+        def make_vT(b):
             vT_b = values.tile([P, LB, H], BF16, name="vT_b")
             for i in range(LB):
                 acc = psum.tile([P, H], F32, name="acc")
                 for c in range(HB):
                     add_to_vT(acc, b, i, c)
                 nc.scalar.activation(vT_b[:, i, :], acc[:], ACT.Silu)
-            z[b], vT[b] = z_b, vT_b
+            vT[b] = vT_b
 
-        def project_z(b):
+        def make_qk(b):
             q_b = sequence.tile([P, HB, L], BF16, name="q_b")
             k_b = sequence.tile([P, HB, L], BF16, name="k_b")
             for d in range(HB):
@@ -207,19 +207,20 @@ def tile_denoisedsasrec_b_kernel(
                 nc.scalar.copy(res_sb[:], acc[:])
                 nc.sync.dma_start(out[e * P : (e + 1) * P, b * L : (b + 1) * L], res_sb[:])
 
-        project_first_x()
+        make_first_z()
+        make_vT(0)
+        make_vT(1)
         build_shared_mask()
-        project_z(0)
-        project_x(1)
-        project_z(1)
-        build_mask(0)
-        scores(0)
-        for b in range(B):
+        make_qk(0)
+        make_qk(1)
+        for b in range(B + 1):
             if b + 2 < B:
-                project_x(b + 2)
-            if b + 1 < B:
-                build_mask(b + 1)
-                scores(b + 1)
+                make_z(b + 2)
+                make_vT(b + 2)
+            if b < B:
+                build_mask(b)
+                scores(b)
             if b + 2 < B:
-                project_z(b + 2)
-            mix(b)
+                make_qk(b + 2)
+            if b >= 1:
+                mix(b - 1)

@@ -65,7 +65,7 @@ def tile_denoisedsasrec_b_kernel(
         def load_column(vector, name):
             tile = held.tile([P, HB], F32, name=name)
             with nc.allow_non_contiguous_dma(reason="512 single floats, one to a partition and block"):
-                nc.gpsimd.dma_start(tile[:], vector.rearrange("(d p) o -> p (d o)", p=P))
+                nc.sync.dma_start(tile[:], vector.rearrange("(d p) o -> p (d o)", p=P))
             return tile
 
         gamma_q_sb = load_column(gamma_q, "gamma_q_sb")
@@ -73,7 +73,7 @@ def tile_denoisedsasrec_b_kernel(
         gamma_k_sb = load_column(gamma_k, "gamma_k_sb")
         beta_k_sb = load_column(beta_k, "beta_k_sb")
         valid_sb = held.tile([P, LB, B], F32, name="valid_sb")
-        nc.gpsimd.dma_start(valid_sb[:], valid.rearrange("(i p) b -> p i b", p=P))
+        nc.sync.dma_start(valid_sb[:], valid.rearrange("(i p) b -> p i b", p=P))
 
         x = [inputs.tile([P, HB, L], BF16, name="x") for b in range(B)]
         for c in range(HB):

@@ -1,4 +1,5 @@
 import concourse.mybir as mybir
+from concourse.masks import make_identity
 
 F32 = mybir.dt.float32
 BF16 = mybir.dt.bfloat16
@@ -13,6 +14,7 @@ N = B * L
 HB = H // P
 LB = L // P
 TEMP = 0.2
+ROOT = (L * H) ** -0.5
 
 WIDTH = [L - i * P for i in range(LB)]
 START = [sum(WIDTH[:i]) for i in range(LB)]
@@ -21,6 +23,10 @@ PACKED = sum(WIDTH)
 
 def block(packed_tile, i):
     return packed_tile[:, START[i] : START[i] + WIDTH[i]]
+
+
+def crossed(packed_tile, i):
+    return packed_tile[:, START[i] : START[i] + P]
 
 
 FLOPS = 4 * 2 * H * H * N + 2 * 2 * H * B * (L * (L + 1) // 2)
@@ -33,9 +39,8 @@ def tile_denoisedsasrec_b_kernel(
     with (
         tc.tile_pool(name="held", bufs=1) as held,
         tc.tile_pool(name="summed", bufs=4) as summed,
-        tc.tile_pool(name="inputs", bufs=B) as inputs,
+        tc.tile_pool(name="every", bufs=B) as every,
         tc.tile_pool(name="sequence", bufs=2) as sequence,
-        tc.tile_pool(name="values", bufs=B) as values,
         tc.tile_pool(name="maskwork", bufs=4) as maskwork,
         tc.tile_pool(name="staging", bufs=4) as staging,
         tc.psum_pool(name="psum", bufs=8) as psum,
@@ -59,8 +64,8 @@ def tile_denoisedsasrec_b_kernel(
         for c in range(1, HB):
             load_table_block(c)
         wv_sb = load_weight(wv, "wv_sb")
-        wq_sb = load_weight(wq, "wq_sb")
         wk_sb = load_weight(wk, "wk_sb")
+        wq_sb = load_weight(wq, "wq_sb")
 
         def load_column(vector, name):
             tile = held.tile([P, HB], F32, name=name)
@@ -75,7 +80,7 @@ def tile_denoisedsasrec_b_kernel(
         valid_sb = held.tile([P, LB, B], F32, name="valid_sb")
         nc.sync.dma_start(valid_sb[:], valid.rearrange("(i p) b -> p i b", p=P))
 
-        x = [inputs.tile([P, HB, L], BF16, name="x") for b in range(B)]
+        x = [every.tile([P, HB, L], BF16, name="x") for b in range(B)]
         for c in range(HB):
             for b in range(B):
                 x_f32 = summed.tile([P, L], F32, name="x_f32")
@@ -83,15 +88,78 @@ def tile_denoisedsasrec_b_kernel(
                 nc.vector.tensor_tensor(x_f32[:], picked, pos[c][:], ALU.add)
                 nc.scalar.copy(x[b][:, c, :], x_f32[:])
 
-        distance = held.tile([P, PACKED], I32, name="distance")
-        is_above = held.tile([P, PACKED], F32, name="is_above")
-        is_diagonal = held.tile([P, PACKED], F32, name="is_diagonal")
-        for i in range(LB):
-            nc.gpsimd.iota(block(distance, i), pattern=[[1, WIDTH[i]]], base=0, channel_multiplier=-1)
+        identity = held.tile([P, P], BF16, name="identity")
+        make_identity(nc, identity[:])
+        ones = held.tile([P, P], BF16, name="ones")
+        nc.gpsimd.memset(ones[:], 1.0)
+        distance = held.tile([P, P], I32, name="distance")
+        nc.gpsimd.iota(distance[:], pattern=[[1, P]], base=0, channel_multiplier=-1)
+        is_above = held.tile([P, P], F32, name="is_above")
         nc.vector.tensor_scalar(is_above[:], distance[:], 0.0, None, ALU.is_gt)
+        is_diagonal = held.tile([P, P], F32, name="is_diagonal")
         nc.vector.tensor_scalar(is_diagonal[:], distance[:], 0.0, None, ALU.is_equal)
+
+        def transposed(weight_sb, name):
+            flipped = held.tile([P, HB, H], BF16, name=name)
+            for first in range(0, HB, 2):
+                bank = psum.tile([P, 2, H], BF16, name="flipped_ps", tag="acc")
+                for j in range(2):
+                    d = first + j
+                    for e in range(HB):
+                        nc.tensor.transpose(
+                            bank[:, j, e * P : (e + 1) * P], weight_sb[:, e, d * P : (d + 1) * P], identity[:]
+                        )
+                nc.vector.tensor_copy(flipped[:, first : first + 2, :], bank[:])
+            return flipped
+
+        def product_over_root(first, second, dtype, name):
+            tile = held.tile([P, HB], dtype, name=name)
+            nc.vector.scalar_tensor_tensor(tile[:], first[:], ROOT, second[:], ALU.mult, ALU.mult)
+            return tile
+
+        fold = held.tile([P, HB, H], BF16, name="fold")
+        key_shift = held.tile([P, HB], F32, name="key_shift")
+        lift_weight = held.tile([P, HB], BF16, name="lift_weight")
+        base = held.tile([P, 1], F32, name="base")
+
+        def fold_weights(wkT, wqT):
+            gains = product_over_root(gamma_k_sb, gamma_q_sb, F32, "gains")
+            wqT_gained = held.tile([P, HB, H], BF16, name="wqT_gained")
+            for d in range(HB):
+                nc.vector.tensor_scalar(wqT_gained[:, d, :], wqT[:, d, :], gains[:, d : d + 1], None, ALU.mult)
+            for e in range(HB):
+                acc = psum.tile([P, H], F32, name="acc")
+                for d in range(HB):
+                    nc.tensor.matmul(
+                        acc[:], wkT[:, d, e * P : (e + 1) * P], wqT_gained[:, d, :], start=(d == 0), stop=(d == HB - 1)
+                    )
+                nc.vector.tensor_copy(fold[:, e, :], acc[:])
+
+            gain_k_shift_q = product_over_root(gamma_k_sb, beta_q_sb, BF16, "gain_k_shift_q")
+            gain_q_shift_k = product_over_root(gamma_q_sb, beta_k_sb, BF16, "gain_q_shift_k")
+            shifts = product_over_root(beta_k_sb, beta_q_sb, BF16, "shifts")
+            acc = psum.tile([P, H], F32, name="acc")
+            for flipped, vector, first in ((wkT, gain_k_shift_q, 0), (wqT, gain_q_shift_k, HB)):
+                for e in range(HB):
+                    for d in range(HB):
+                        nc.tensor.matmul(
+                            acc[:, first + e : first + e + 1],
+                            flipped[:, d, e * P : (e + 1) * P],
+                            vector[:, d : d + 1],
+                            start=(d == 0),
+                            stop=(d == HB - 1),
+                        )
+            for d in range(HB):
+                nc.tensor.matmul(
+                    acc[:, 2 * HB : 2 * HB + 1], ones[:], shifts[:, d : d + 1], start=(d == 0), stop=(d == HB - 1)
+                )
+            nc.vector.tensor_copy(lift_weight[:], acc[:, 0:HB])
+            nc.vector.tensor_copy(key_shift[:], acc[:, HB : 2 * HB])
+            nc.vector.tensor_copy(base[:], acc[:, 2 * HB : 2 * HB + 1])
+
         above = held.tile([P, PACKED], F32, name="above")
         diagonal = held.tile([P, PACKED], F32, name="diagonal")
+        nc.gpsimd.memset(diagonal[:], 0.0)
 
         def build_shared_mask():
             def step(name):
@@ -111,18 +179,15 @@ def tile_denoisedsasrec_b_kernel(
             nc.vector.tensor_add(noisy[:], ln_w[:], g_sb[:])
             logit = step("logit")
             nc.vector.tensor_sub(logit[:], noisy[:], ln_rest[:])
-            smask = step("smask")
-            nc.scalar.activation(smask[:], logit[:], ACT.Sigmoid, scale=1.0 / TEMP)
-            nc.vector.tensor_mul(above[:], smask[:], is_above[:])
-            nc.vector.tensor_mul(diagonal[:], smask[:], is_diagonal[:])
+            nc.scalar.activation(above[:], logit[:], ACT.Sigmoid, scale=1.0 / TEMP)
+            for i in range(LB):
+                nc.vector.tensor_mul(crossed(diagonal, i), crossed(above, i), is_diagonal[:])
+                nc.vector.tensor_mul(crossed(above, i), crossed(above, i), is_above[:])
 
-        z, vT, q, k, mask, p = {}, {}, {}, {}, {}, {}
+        z, vT, key, lift, mask, p = {}, {}, {}, {}, {}, {}
 
         def add_to_z(acc, b, e, c):
             nc.tensor.matmul(acc[:], wz_sb[:, c, e * P : (e + 1) * P], x[b][:, c, :], start=(c == 0), stop=(c == HB - 1))
-
-        def add_to_vT(acc, b, i, c):
-            nc.tensor.matmul(acc[:], x[b][:, c, i * P : (i + 1) * P], wv_sb[:, c, :], start=(c == 0), stop=(c == HB - 1))
 
         def make_first_z():
             first = range(2)
@@ -132,13 +197,13 @@ def tile_denoisedsasrec_b_kernel(
                     for e in range(HB):
                         add_to_z(z_acc[b][e], b, e, c)
             for b in first:
-                z_b = sequence.tile([P, HB, L], BF16, name="z_b")
+                z_b = every.tile([P, HB, L], BF16, name="z_b")
                 for e in range(HB):
                     nc.scalar.activation(z_b[:, e, :], z_acc[b][e][:], ACT.Silu)
                 z[b] = z_b
 
         def make_z(b):
-            z_b = sequence.tile([P, HB, L], BF16, name="z_b")
+            z_b = every.tile([P, HB, L], BF16, name="z_b")
             for e in range(HB):
                 acc = psum.tile([P, L], F32, name="acc")
                 for c in range(HB):
@@ -147,31 +212,38 @@ def tile_denoisedsasrec_b_kernel(
             z[b] = z_b
 
         def make_vT(b):
-            vT_b = values.tile([P, LB, H], BF16, name="vT_b")
+            vT_b = every.tile([P, LB, H], BF16, name="vT_b")
             for i in range(LB):
                 acc = psum.tile([P, H], F32, name="acc")
                 for c in range(HB):
-                    add_to_vT(acc, b, i, c)
+                    nc.tensor.matmul(
+                        acc[:], x[b][:, c, i * P : (i + 1) * P], wv_sb[:, c, :], start=(c == 0), stop=(c == HB - 1)
+                    )
                 nc.scalar.activation(vT_b[:, i, :], acc[:], ACT.Silu)
             vT[b] = vT_b
 
-        def make_qk(b):
-            q_b = sequence.tile([P, HB, L], BF16, name="q_b")
-            k_b = sequence.tile([P, HB, L], BF16, name="k_b")
-            for d in range(HB):
-                for weight, gamma, beta, result in (
-                    (wq_sb, gamma_q_sb, beta_q_sb, q_b),
-                    (wk_sb, gamma_k_sb, beta_k_sb, k_b),
-                ):
-                    acc = psum.tile([P, L], F32, name="acc")
-                    for e in range(HB):
-                        nc.tensor.matmul(
-                            acc[:], weight[:, e, d * P : (d + 1) * P], z[b][:, e, :], start=(e == 0), stop=(e == HB - 1)
-                        )
-                    nc.vector.tensor_scalar(
-                        result[:, d, :], acc[:], gamma[:, d : d + 1], beta[:, d : d + 1], ALU.mult, ALU.add
+        def make_key(b):
+            key_b = sequence.tile([P, HB, L], BF16, name="key_b")
+            for f in range(HB):
+                acc = psum.tile([P, L], F32, name="acc")
+                for e in range(HB):
+                    nc.tensor.matmul(
+                        acc[:], fold[:, e, f * P : (f + 1) * P], z[b][:, e, :], start=(e == 0), stop=(e == HB - 1)
                     )
-            q[b], k[b] = q_b, k_b
+                nc.vector.tensor_scalar(key_b[:, f, :], acc[:], key_shift[:, f : f + 1], None, ALU.add)
+            acc = psum.tile([P, L], F32, name="acc")
+            for i in range(LB):
+                for e in range(HB):
+                    nc.tensor.matmul(
+                        acc[:, i : i + 1],
+                        z[b][:, e, i * P : (i + 1) * P],
+                        lift_weight[:, e : e + 1],
+                        start=(e == 0),
+                        stop=(e == HB - 1),
+                    )
+            lift_b = sequence.tile([P, LB], F32, name="lift_b")
+            nc.vector.tensor_scalar(lift_b[:], acc[:, 0:LB], base[:, 0:1], None, ALU.add)
+            key[b], lift[b] = key_b, lift_b
 
         def build_mask(b):
             mask_b = sequence.tile([P, PACKED], F32, name="mask_b")
@@ -182,45 +254,48 @@ def tile_denoisedsasrec_b_kernel(
             mask[b] = mask_b
 
         def scores(b):
-            p_b = sequence.tile([P, LB, L], BF16, name="p_b")
+            masked = sequence.tile([P, PACKED], F32, name="masked")
             for i in range(LB):
                 cols = slice(i * P, L)
                 acc = psum.tile([P, L], F32, name="acc")
-                for d in range(HB):
+                for f in range(HB):
                     nc.tensor.matmul(
-                        acc[:, cols], k[b][:, d, i * P : (i + 1) * P], q[b][:, d, cols], start=(d == 0), stop=(d == HB - 1)
+                        acc[:, cols], key[b][:, f, i * P : (i + 1) * P], z[b][:, f, cols], start=(f == 0), stop=(f == HB - 1)
                     )
-                kept = staging.tile([P, L], F32, name="kept")
-                nc.vector.scalar_tensor_tensor(kept[:, cols], acc[:, cols], 0.0, block(mask[b], i), ALU.max, ALU.mult)
-                nc.scalar.activation(p_b[:, i, cols], kept[:, cols], ACT.Square, scale=(L * H) ** -0.5)
+                nc.vector.scalar_tensor_tensor(
+                    block(masked, i), acc[:, cols], lift[b][:, i : i + 1], block(mask[b], i), ALU.add, ALU.mult
+                )
+            p_b = sequence.tile([P, PACKED], BF16, name="p_b")
+            nc.vector.scalar_tensor_tensor(p_b[:], masked[:], 0.0, masked[:], ALU.max, ALU.mult)
             p[b] = p_b
 
         def mix(b):
             for e in range(HB):
                 acc = psum.tile([P, L], F32, name="acc")
                 for i in range(LB):
-                    cols = slice(i * P, L)
                     nc.tensor.matmul(
-                        acc[:, cols], vT[b][:, i, e * P : (e + 1) * P], p[b][:, i, cols], start=(i == 0), stop=(i == LB - 1)
+                        acc[:, i * P : L], vT[b][:, i, e * P : (e + 1) * P], block(p[b], i), start=(i == 0), stop=(i == LB - 1)
                     )
                 res_sb = staging.tile([P, L], F32, name="res_sb")
                 nc.scalar.copy(res_sb[:], acc[:])
                 nc.sync.dma_start(out[e * P : (e + 1) * P, b * L : (b + 1) * L], res_sb[:])
 
         make_first_z()
-        make_vT(0)
-        make_vT(1)
-        build_shared_mask()
-        make_qk(0)
-        make_qk(1)
-        for b in range(B + 1):
-            if b + 2 < B:
-                make_z(b + 2)
-                make_vT(b + 2)
-            if b < B:
-                build_mask(b)
-                scores(b)
-            if b + 2 < B:
-                make_qk(b + 2)
-            if b >= 1:
-                mix(b - 1)
+        for s in range(B + 4):
+            if 2 <= s < B:
+                make_z(s)
+            if s < B:
+                make_vT(s)
+            if s == 0:
+                wkT = transposed(wk_sb, "wkT")
+                wqT = transposed(wq_sb, "wqT")
+            if s == 1:
+                fold_weights(wkT, wqT)
+                build_shared_mask()
+            if 0 <= s - 2 < B:
+                make_key(s - 2)
+                build_mask(s - 2)
+            if 0 <= s - 3 < B:
+                scores(s - 3)
+            if 0 <= s - 4 < B:
+                mix(s - 4)

@@ -59,34 +59,29 @@ def tile_denoisedsasrec_b_kernel(
             nc.sync.dma_start(pos[c][:], pos_emb[c * P : (c + 1) * P, :])
             nc.sync.dma_start(table[c][:], item_emb[c * P : (c + 1) * P, :])
 
-        load_table_block(0)
-        wz_sb = load_weight(wz, "wz_sb")
-        for c in range(1, HB):
-            load_table_block(c)
-        wv_sb = load_weight(wv, "wv_sb")
-        wk_sb = load_weight(wk, "wk_sb")
-        wq_sb = load_weight(wq, "wq_sb")
-
         def load_column(vector, name):
             tile = held.tile([P, HB], F32, name=name)
             with nc.allow_non_contiguous_dma(reason="512 single floats, one to a partition and block"):
-                nc.sync.dma_start(tile[:], vector.rearrange("(d p) o -> p (d o)", p=P))
+                nc.scalar.dma_start(tile[:], vector.rearrange("(d p) o -> p (d o)", p=P))
             return tile
 
         gamma_q_sb = load_column(gamma_q, "gamma_q_sb")
         beta_q_sb = load_column(beta_q, "beta_q_sb")
         gamma_k_sb = load_column(gamma_k, "gamma_k_sb")
         beta_k_sb = load_column(beta_k, "beta_k_sb")
+        wk_sb = load_weight(wk, "wk_sb")
+        wq_sb = load_weight(wq, "wq_sb")
+        load_table_block(0)
+        wz_sb = load_weight(wz, "wz_sb")
+        for c in range(1, HB):
+            load_table_block(c)
+        wv_sb = load_weight(wv, "wv_sb")
         valid_sb = held.tile([P, LB, B], F32, name="valid_sb")
         nc.sync.dma_start(valid_sb[:], valid.rearrange("(i p) b -> p i b", p=P))
 
-        x = [every.tile([P, HB, L], BF16, name="x") for b in range(B)]
-        for c in range(HB):
-            for b in range(B):
-                x_f32 = summed.tile([P, L], F32, name="x_f32")
-                picked = table[c][:].indirect(offsets[:, b * (L // 16) : (b + 1) * (L // 16)])
-                nc.vector.tensor_tensor(x_f32[:], picked, pos[c][:], ALU.add)
-                nc.scalar.copy(x[b][:, c, :], x_f32[:])
+        warm_up = held.tile([P, 1], F32, name="warm_up")
+        nc.gpsimd.memset(warm_up[:], 0.0)
+        nc.scalar.activation(warm_up[:], warm_up[:], ACT.Silu)
 
         identity = held.tile([P, P], BF16, name="identity")
         make_identity(nc, identity[:])
@@ -99,47 +94,39 @@ def tile_denoisedsasrec_b_kernel(
         is_diagonal = held.tile([P, P], F32, name="is_diagonal")
         nc.vector.tensor_scalar(is_diagonal[:], distance[:], 0.0, None, ALU.is_equal)
 
-        def transposed(weight_sb, name):
+        def flipped_and_gained(weight_sb, gain, name):
             flipped = held.tile([P, HB, H], BF16, name=name)
-            for first in range(0, HB, 2):
-                bank = psum.tile([P, 2, H], BF16, name="flipped_ps", tag="acc")
-                for j in range(2):
-                    d = first + j
-                    for e in range(HB):
-                        nc.tensor.transpose(
-                            bank[:, j, e * P : (e + 1) * P], weight_sb[:, e, d * P : (d + 1) * P], identity[:]
-                        )
-                nc.vector.tensor_copy(flipped[:, first : first + 2, :], bank[:])
+            for d in range(HB):
+                bank = psum.tile([P, H], BF16, name="flipped_ps", tag="acc")
+                for e in range(HB):
+                    nc.tensor.transpose(bank[:, e * P : (e + 1) * P], weight_sb[:, e, d * P : (d + 1) * P], identity[:])
+                nc.scalar.activation(flipped[:, d, :], bank[:], ACT.Copy, scale=gain[:, d : d + 1])
             return flipped
-
-        def product_over_root(first, second, dtype, name):
-            tile = held.tile([P, HB], dtype, name=name)
-            nc.vector.scalar_tensor_tensor(tile[:], first[:], ROOT, second[:], ALU.mult, ALU.mult)
-            return tile
 
         fold = held.tile([P, HB, H], BF16, name="fold")
         key_shift = held.tile([P, HB], F32, name="key_shift")
         lift_weight = held.tile([P, HB], BF16, name="lift_weight")
         base = held.tile([P, 1], F32, name="base")
 
-        def fold_weights(wkT, wqT):
-            gains = product_over_root(gamma_k_sb, gamma_q_sb, F32, "gains")
-            wqT_gained = held.tile([P, HB, H], BF16, name="wqT_gained")
-            for d in range(HB):
-                nc.vector.tensor_scalar(wqT_gained[:, d, :], wqT[:, d, :], gains[:, d : d + 1], None, ALU.mult)
+        def fold_weights():
+            gamma_k_rooted = held.tile([P, HB], F32, name="gamma_k_rooted")
+            nc.vector.tensor_scalar(gamma_k_rooted[:], gamma_k_sb[:], ROOT, None, ALU.mult)
+            wkT = flipped_and_gained(wk_sb, gamma_k_rooted, "wkT")
+            wqT = flipped_and_gained(wq_sb, gamma_q_sb, "wqT")
             for e in range(HB):
                 acc = psum.tile([P, H], F32, name="acc")
                 for d in range(HB):
-                    nc.tensor.matmul(
-                        acc[:], wkT[:, d, e * P : (e + 1) * P], wqT_gained[:, d, :], start=(d == 0), stop=(d == HB - 1)
-                    )
-                nc.vector.tensor_copy(fold[:, e, :], acc[:])
+                    nc.tensor.matmul(acc[:], wkT[:, d, e * P : (e + 1) * P], wqT[:, d, :], start=(d == 0), stop=(d == HB - 1))
+                nc.scalar.copy(fold[:, e, :], acc[:])
 
-            gain_k_shift_q = product_over_root(gamma_k_sb, beta_q_sb, BF16, "gain_k_shift_q")
-            gain_q_shift_k = product_over_root(gamma_q_sb, beta_k_sb, BF16, "gain_q_shift_k")
-            shifts = product_over_root(beta_k_sb, beta_q_sb, BF16, "shifts")
+            shift_q = held.tile([P, HB], BF16, name="shift_q")
+            nc.vector.tensor_copy(shift_q[:], beta_q_sb[:])
+            shift_k_rooted = held.tile([P, HB], BF16, name="shift_k_rooted")
+            nc.vector.tensor_scalar(shift_k_rooted[:], beta_k_sb[:], ROOT, None, ALU.mult)
+            shifts_rooted = held.tile([P, HB], BF16, name="shifts_rooted")
+            nc.vector.scalar_tensor_tensor(shifts_rooted[:], beta_k_sb[:], ROOT, beta_q_sb[:], ALU.mult, ALU.mult)
             acc = psum.tile([P, H], F32, name="acc")
-            for flipped, vector, first in ((wkT, gain_k_shift_q, 0), (wqT, gain_q_shift_k, HB)):
+            for flipped, vector, first in ((wkT, shift_q, 0), (wqT, shift_k_rooted, HB)):
                 for e in range(HB):
                     for d in range(HB):
                         nc.tensor.matmul(
@@ -151,11 +138,21 @@ def tile_denoisedsasrec_b_kernel(
                         )
             for d in range(HB):
                 nc.tensor.matmul(
-                    acc[:, 2 * HB : 2 * HB + 1], ones[:], shifts[:, d : d + 1], start=(d == 0), stop=(d == HB - 1)
+                    acc[:, 2 * HB : 2 * HB + 1], ones[:], shifts_rooted[:, d : d + 1], start=(d == 0), stop=(d == HB - 1)
                 )
-            nc.vector.tensor_copy(lift_weight[:], acc[:, 0:HB])
-            nc.vector.tensor_copy(key_shift[:], acc[:, HB : 2 * HB])
-            nc.vector.tensor_copy(base[:], acc[:, 2 * HB : 2 * HB + 1])
+            nc.scalar.copy(lift_weight[:], acc[:, 0:HB])
+            nc.scalar.copy(key_shift[:], acc[:, HB : 2 * HB])
+            nc.scalar.copy(base[:], acc[:, 2 * HB : 2 * HB + 1])
+
+        fold_weights()
+
+        x = [every.tile([P, HB, L], BF16, name="x") for b in range(B)]
+        for c in range(HB):
+            for b in range(B):
+                x_f32 = summed.tile([P, L], F32, name="x_f32")
+                picked = table[c][:].indirect(offsets[:, b * (L // 16) : (b + 1) * (L // 16)])
+                nc.vector.tensor_tensor(x_f32[:], picked, pos[c][:], ALU.add)
+                nc.scalar.copy(x[b][:, c, :], x_f32[:])
 
         above = held.tile([P, PACKED], F32, name="above")
         diagonal = held.tile([P, PACKED], F32, name="diagonal")
@@ -280,22 +277,27 @@ def tile_denoisedsasrec_b_kernel(
                 nc.scalar.copy(res_sb[:], acc[:])
                 nc.sync.dma_start(out[e * P : (e + 1) * P, b * L : (b + 1) * L], res_sb[:])
 
+        first_pair, second_pair = (0, 1), (2, 3)
         make_first_z()
-        for s in range(B + 4):
-            if 2 <= s < B:
-                make_z(s)
-            if s < B:
-                make_vT(s)
-            if s == 0:
-                wkT = transposed(wk_sb, "wkT")
-                wqT = transposed(wq_sb, "wqT")
-            if s == 1:
-                fold_weights(wkT, wqT)
-                build_shared_mask()
-            if 0 <= s - 2 < B:
-                make_key(s - 2)
-                build_mask(s - 2)
-            if 0 <= s - 3 < B:
-                scores(s - 3)
-            if 0 <= s - 4 < B:
-                mix(s - 4)
+        make_vT(0)
+        for b in first_pair:
+            make_key(b)
+        build_shared_mask()
+        for b in first_pair:
+            build_mask(b)
+        make_vT(1)
+        for b in second_pair:
+            make_z(b)
+        for b in first_pair:
+            scores(b)
+        for b in second_pair:
+            make_key(b)
+            build_mask(b)
+        for b in first_pair:
+            mix(b)
+        for b in second_pair:
+            make_vT(b)
+        for b in second_pair:
+            scores(b)
+        for b in second_pair:
+            mix(b)

@@ -42,7 +42,7 @@ def tile_denoisedsasrec_b_kernel(
         tc.tile_pool(name="every", bufs=B) as every,
         tc.tile_pool(name="sequence", bufs=2) as sequence,
         tc.tile_pool(name="maskwork", bufs=4) as maskwork,
-        tc.tile_pool(name="staging", bufs=4) as staging,
+        tc.tile_pool(name="staging", bufs=6) as staging,
         tc.psum_pool(name="psum", bufs=8) as psum,
     ):
         def load_weight(weight, name):
@@ -55,9 +55,13 @@ def tile_denoisedsasrec_b_kernel(
         table = [held.tile([P, S], F32, name=f"table{c}") for c in range(HB)]
         pos = [held.tile([P, L], F32, name=f"pos{c}") for c in range(HB)]
 
+        wz_sb = held.tile([P, HB, H], BF16, name="wz_sb")
+
         def load_table_block(c):
-            nc.sync.dma_start(pos[c][:], pos_emb[c * P : (c + 1) * P, :])
-            nc.sync.dma_start(table[c][:], item_emb[c * P : (c + 1) * P, :])
+            rows = slice(c * P, (c + 1) * P)
+            nc.sync.dma_start(pos[c][:], pos_emb[rows, :])
+            nc.sync.dma_start(table[c][:], item_emb[rows, :])
+            nc.sync.dma_start(wz_sb[:, c, :], wz[rows, :])
 
         def load_column(vector, name):
             tile = held.tile([P, HB], F32, name=name)
@@ -71,9 +75,7 @@ def tile_denoisedsasrec_b_kernel(
         beta_k_sb = load_column(beta_k, "beta_k_sb")
         wk_sb = load_weight(wk, "wk_sb")
         wq_sb = load_weight(wq, "wq_sb")
-        load_table_block(0)
-        wz_sb = load_weight(wz, "wz_sb")
-        for c in range(1, HB):
+        for c in range(HB):
             load_table_block(c)
         wv_sb = load_weight(wv, "wv_sb")
         valid_sb = held.tile([P, LB, B], F32, name="valid_sb")

@@ -15,6 +15,7 @@ HB = H // P
 LB = L // P
 TEMP = 0.2
 ROOT = (L * H) ** -0.5
+FLIPPED_ROWS = 64
 
 WIDTH = [L - i * P for i in range(LB)]
 START = [sum(WIDTH[:i]) for i in range(LB)]
@@ -63,16 +64,10 @@ def tile_denoisedsasrec_b_kernel(
             nc.sync.dma_start(table[c][:], item_emb[rows, :])
             nc.sync.dma_start(wz_sb[:, c, :], wz[rows, :])
 
-        def load_column(vector, name):
-            tile = held.tile([P, HB], F32, name=name)
-            with nc.allow_non_contiguous_dma(reason="512 single floats, one to a partition and block"):
-                nc.scalar.dma_start(tile[:], vector.rearrange("(d p) o -> p (d o)", p=P))
-            return tile
-
-        gamma_q_sb = load_column(gamma_q, "gamma_q_sb")
-        beta_q_sb = load_column(beta_q, "beta_q_sb")
-        gamma_k_sb = load_column(gamma_k, "gamma_k_sb")
-        beta_k_sb = load_column(beta_k, "beta_k_sb")
+        vector_rows = held.tile([FLIPPED_ROWS, P], F32, name="vector_rows")
+        nc.gpsimd.memset(vector_rows[:], 0.0)
+        for k, vector in enumerate((gamma_q, beta_q, gamma_k, beta_k)):
+            nc.sync.dma_start(vector_rows[k * HB : (k + 1) * HB, :], vector.rearrange("(d p) o -> d (p o)", p=P))
         wk_sb = load_weight(wk, "wk_sb")
         wq_sb = load_weight(wq, "wq_sb")
         for c in range(HB):
@@ -96,6 +91,14 @@ def tile_denoisedsasrec_b_kernel(
         is_diagonal = held.tile([P, P], F32, name="is_diagonal")
         nc.vector.tensor_scalar(is_diagonal[:], distance[:], 0.0, None, ALU.is_equal)
 
+        identity_f32 = held.tile([FLIPPED_ROWS, FLIPPED_ROWS], F32, name="identity_f32")
+        make_identity(nc, identity_f32[:])
+        vector_columns_ps = psum.tile([P, FLIPPED_ROWS], F32, name="vector_columns_ps", tag="acc")
+        nc.tensor.transpose(vector_columns_ps[:], vector_rows[:], identity_f32[:])
+        vector_columns = held.tile([P, 4 * HB], F32, name="vector_columns")
+        nc.vector.tensor_copy(vector_columns[:], vector_columns_ps[:, 0 : 4 * HB])
+        gamma_q_sb, beta_q_sb, gamma_k_sb, beta_k_sb = [vector_columns[:, k * HB : (k + 1) * HB] for k in range(4)]
+
         def flipped_and_gained(weight_sb, gain, name):
             flipped = held.tile([P, HB, H], BF16, name=name)
             for d in range(HB):
@@ -112,7 +115,7 @@ def tile_denoisedsasrec_b_kernel(
 
         def fold_weights():
             gamma_k_rooted = held.tile([P, HB], F32, name="gamma_k_rooted")
-            nc.vector.tensor_scalar(gamma_k_rooted[:], gamma_k_sb[:], ROOT, None, ALU.mult)
+            nc.vector.tensor_scalar(gamma_k_rooted[:], gamma_k_sb, ROOT, None, ALU.mult)
             wkT = flipped_and_gained(wk_sb, gamma_k_rooted, "wkT")
             wqT = flipped_and_gained(wq_sb, gamma_q_sb, "wqT")
             for e in range(HB):
@@ -122,11 +125,11 @@ def tile_denoisedsasrec_b_kernel(
                 nc.scalar.copy(fold[:, e, :], acc[:])
 
             shift_q = held.tile([P, HB], BF16, name="shift_q")
-            nc.vector.tensor_copy(shift_q[:], beta_q_sb[:])
+            nc.vector.tensor_copy(shift_q[:], beta_q_sb)
             shift_k_rooted = held.tile([P, HB], BF16, name="shift_k_rooted")
-            nc.vector.tensor_scalar(shift_k_rooted[:], beta_k_sb[:], ROOT, None, ALU.mult)
+            nc.vector.tensor_scalar(shift_k_rooted[:], beta_k_sb, ROOT, None, ALU.mult)
             shifts_rooted = held.tile([P, HB], BF16, name="shifts_rooted")
-            nc.vector.scalar_tensor_tensor(shifts_rooted[:], beta_k_sb[:], ROOT, beta_q_sb[:], ALU.mult, ALU.mult)
+            nc.vector.scalar_tensor_tensor(shifts_rooted[:], beta_k_sb, ROOT, beta_q_sb, ALU.mult, ALU.mult)
             acc = psum.tile([P, H], F32, name="acc")
             for flipped, vector, first in ((wkT, shift_q, 0), (wqT, shift_k_rooted, HB)):
                 for e in range(HB):

@@ -110,7 +110,7 @@ def tile_denoisedsasrec_b_kernel(
 
         fold = held.tile([P, HB, H], BF16, name="fold")
         key_shift = held.tile([P, HB], F32, name="key_shift")
-        lift_weight = held.tile([P, HB], BF16, name="lift_weight")
+        lift_weight = held.tile([P, HB], F32, name="lift_weight")
         base = held.tile([P, 1], F32, name="base")
 
         def fold_weights():
@@ -233,16 +233,22 @@ def tile_denoisedsasrec_b_kernel(
                         acc[:], fold[:, e, f * P : (f + 1) * P], z[b][:, e, :], start=(e == 0), stop=(e == HB - 1)
                     )
                 nc.vector.tensor_scalar(key_b[:, f, :], acc[:], key_shift[:, f : f + 1], None, ALU.add)
+            weighted = None
+            for e in range(HB):
+                if e < HB - 1:
+                    total = summed.tile([P, L], F32, name="weighted", tag="x_f32")
+                else:
+                    total = sequence.tile([P, L], BF16, name="weighted_sum")
+                if e == 0:
+                    nc.vector.tensor_scalar(total[:], z[b][:, e, :], lift_weight[:, e : e + 1], None, ALU.mult)
+                else:
+                    nc.vector.scalar_tensor_tensor(
+                        total[:], z[b][:, e, :], lift_weight[:, e : e + 1], weighted[:], ALU.mult, ALU.add
+                    )
+                weighted = total
             acc = psum.tile([P, L], F32, name="acc")
             for i in range(LB):
-                for e in range(HB):
-                    nc.tensor.matmul(
-                        acc[:, i : i + 1],
-                        z[b][:, e, i * P : (i + 1) * P],
-                        lift_weight[:, e : e + 1],
-                        start=(e == 0),
-                        stop=(e == HB - 1),
-                    )
+                nc.tensor.matmul(acc[:, i : i + 1], weighted[:, i * P : (i + 1) * P], ones[:, 0:1], start=True, stop=True)
             lift_b = sequence.tile([P, LB], F32, name="lift_b")
             nc.vector.tensor_scalar(lift_b[:], acc[:, 0:LB], base[:, 0:1], None, ALU.add)
             key[b], lift[b] = key_b, lift_b

@@ -68,8 +68,13 @@ def tile_denoisedsasrec_b_kernel(
         nc.gpsimd.memset(vector_rows[:], 0.0)
         for k, vector in enumerate((gamma_q, beta_q, gamma_k, beta_k)):
             nc.sync.dma_start(vector_rows[k * HB : (k + 1) * HB, :], vector.rearrange("(d p) o -> d (p o)", p=P))
-        wk_sb = load_weight(wk, "wk_sb")
-        wq_sb = load_weight(wq, "wq_sb")
+        def load_weight_whole_rows(weight, name):
+            tile = held.tile([P, HB, H], BF16, name=name)
+            nc.sync.dma_start(tile[:], weight.rearrange("(p j) d -> p j d", j=HB))
+            return tile
+
+        wk_sb = load_weight_whole_rows(wk, "wk_sb")
+        wq_sb = load_weight_whole_rows(wq, "wq_sb")
         for c in range(HB):
             load_table_block(c)
         wv_sb = load_weight(wv, "wv_sb")
@@ -189,7 +194,7 @@ def tile_denoisedsasrec_b_kernel(
         z, vT, key, lift, mask, p = {}, {}, {}, {}, {}, {}
 
         def add_to_z(acc, b, e, c):
-            nc.tensor.matmul(acc[:], wz_sb[:, c, e * P : (e + 1) * P], x[b][:, c, :], start=(c == 0), stop=(c == HB - 1))
+            nc.tensor.matmul(acc[:], wz_sb[:, c, e::HB], x[b][:, c, :], start=(c == 0), stop=(c == HB - 1))
 
         def make_first_z():
             first = range(2)

@@ -21,6 +21,9 @@ WIDTH = [L - i * P for i in range(LB)]
 START = [sum(WIDTH[:i]) for i in range(LB)]
 PACKED = sum(WIDTH)
 
+KEPT = 6
+PARKED_PER_BLOCK = 4
+
 
 def block(packed_tile, i):
     return packed_tile[:, START[i] : START[i] + WIDTH[i]]
@@ -39,6 +42,7 @@ def tile_denoisedsasrec_b_kernel(
     nc = tc.nc
     with (
         tc.tile_pool(name="held", bufs=1) as held,
+        tc.tile_pool(name="early", bufs=4) as early,
         tc.tile_pool(name="summed", bufs=4) as summed,
         tc.tile_pool(name="every", bufs=B) as every,
         tc.tile_pool(name="sequence", bufs=2) as sequence,
@@ -69,7 +73,7 @@ def tile_denoisedsasrec_b_kernel(
         for k, vector in enumerate((gamma_q, beta_q, gamma_k, beta_k)):
             nc.sync.dma_start(vector_rows[k * HB : (k + 1) * HB, :], vector.rearrange("(d p) o -> d (p o)", p=P))
         def load_weight_whole_rows(weight, name):
-            tile = held.tile([P, HB, H], BF16, name=name)
+            tile = early.tile([P, HB, H], BF16, name=name, tag="early")
             nc.sync.dma_start(tile[:], weight.rearrange("(p j) d -> p j d", j=HB))
             return tile
 
@@ -105,7 +109,7 @@ def tile_denoisedsasrec_b_kernel(
         gamma_q_sb, beta_q_sb, gamma_k_sb, beta_k_sb = [vector_columns[:, k * HB : (k + 1) * HB] for k in range(4)]
 
         def flipped_and_gained(weight_sb, gain, name):
-            flipped = held.tile([P, HB, H], BF16, name=name)
+            flipped = early.tile([P, HB, H], BF16, name=name, tag="early")
             for d in range(HB):
                 bank = psum.tile([P, H], BF16, name="flipped_ps", tag="acc")
                 for e in range(HB):
@@ -157,12 +161,12 @@ def tile_denoisedsasrec_b_kernel(
         fold_weights()
 
         x = [every.tile([P, HB, L], BF16, name="x") for b in range(B)]
-        for c in range(HB):
-            for b in range(B):
-                x_f32 = summed.tile([P, L], F32, name="x_f32")
-                picked = table[c][:].indirect(offsets[:, b * (L // 16) : (b + 1) * (L // 16)])
-                nc.vector.tensor_tensor(x_f32[:], picked, pos[c][:], ALU.add)
-                nc.scalar.copy(x[b][:, c, :], x_f32[:])
+
+        def look_up(c, b):
+            x_f32 = summed.tile([P, L], F32, name="x_f32")
+            picked = table[c][:].indirect(offsets[:, b * (L // 16) : (b + 1) * (L // 16)])
+            nc.vector.tensor_tensor(x_f32[:], picked, pos[c][:], ALU.add)
+            nc.scalar.copy(x[b][:, c, :], x_f32[:])
 
         above = held.tile([P, PACKED], F32, name="above")
         diagonal = held.tile([P, PACKED], F32, name="diagonal")
@@ -192,30 +196,51 @@ def tile_denoisedsasrec_b_kernel(
                 nc.vector.tensor_mul(crossed(above, i), crossed(above, i), is_above[:])
 
         z, vT, key, lift, mask, p = {}, {}, {}, {}, {}, {}
+        lift_all = held.tile([P, B, LB], F32, name="lift_all")
 
-        def add_to_z(acc, b, e, c):
-            nc.tensor.matmul(acc[:], wz_sb[:, c, e::HB], x[b][:, c, :], start=(c == 0), stop=(c == HB - 1))
+        def add_to_z(acc, b, e, c, first, last):
+            nc.tensor.matmul(acc[:], wz_sb[:, c, e::HB], x[b][:, c, :], start=(c == first), stop=(c == last))
 
-        def make_first_z():
-            first = range(2)
-            z_acc = [[psum.tile([P, L], F32, name="acc") for e in range(HB)] for b in first]
+        z_sums = [(b, e) for b in range(B) for e in range(HB)]
+        kept = {}
+        parked = {}
+
+        def look_up_and_begin_z():
+            for b, e in z_sums[:KEPT]:
+                kept[(b, e)] = psum.tile([P, L], F32, name="acc")
             for c in range(HB):
-                for b in first:
-                    for e in range(HB):
-                        add_to_z(z_acc[b][e], b, e, c)
-            for b in first:
-                z_b = every.tile([P, HB, L], BF16, name="z_b")
-                for e in range(HB):
-                    nc.scalar.activation(z_b[:, e, :], z_acc[b][e][:], ACT.Silu)
-                z[b] = z_b
+                to_park = []
+                if 1 <= c <= HB - 2:
+                    to_park = z_sums[KEPT + (c - 1) * PARKED_PER_BLOCK : KEPT + c * PARKED_PER_BLOCK]
+                urgent = [b for b, e in to_park]
+                for b in sorted(range(B), key=lambda b: b not in urgent):
+                    look_up(c, b)
+                for k, (b, e) in enumerate(to_park):
+                    if k % 2 == 0:
+                        pair = early.tile([P, 2, L], F32, name="pair", tag="early")
+                    acc = psum.tile([P, L], F32, name="acc")
+                    for earlier in range(c + 1):
+                        add_to_z(acc, b, e, earlier, 0, c)
+                    nc.scalar.copy(pair[:, k % 2, :], acc[:])
+                    parked[(b, e)] = (pair[:, k % 2, :], c + 1)
+                for b, e in z_sums[:KEPT]:
+                    add_to_z(kept[(b, e)], b, e, c, 0, HB - 1)
 
-        def make_z(b):
+        def finish_z(b):
             z_b = every.tile([P, HB, L], BF16, name="z_b")
             for e in range(HB):
-                acc = psum.tile([P, L], F32, name="acc")
-                for c in range(HB):
-                    add_to_z(acc, b, e, c)
-                nc.scalar.activation(z_b[:, e, :], acc[:], ACT.Silu)
+                if (b, e) in kept:
+                    whole = kept[(b, e)]
+                else:
+                    share, begun = parked.get((b, e), (None, 0))
+                    whole = psum.tile([P, L], F32, name="acc")
+                    for c in range(begun, HB):
+                        add_to_z(whole, b, e, c, begun, HB - 1)
+                    if begun > 0:
+                        rest = whole
+                        whole = summed.tile([P, L], F32, name="whole", tag="x_f32")
+                        nc.vector.tensor_tensor(whole[:], rest[:], share, ALU.add)
+                nc.scalar.activation(z_b[:, e, :], whole[:], ACT.Silu)
             z[b] = z_b
 
         def make_vT(b):
@@ -230,7 +255,7 @@ def tile_denoisedsasrec_b_kernel(
             vT[b] = vT_b
 
         def make_key(b):
-            key_b = sequence.tile([P, HB, L], BF16, name="key_b")
+            key_b = every.tile([P, HB, L], BF16, name="key_b", tag="x")
             for f in range(HB):
                 acc = psum.tile([P, L], F32, name="acc")
                 for e in range(HB):
@@ -254,12 +279,12 @@ def tile_denoisedsasrec_b_kernel(
             acc = psum.tile([P, L], F32, name="acc")
             for i in range(LB):
                 nc.tensor.matmul(acc[:, i : i + 1], weighted[:, i * P : (i + 1) * P], ones[:, 0:1], start=True, stop=True)
-            lift_b = sequence.tile([P, LB], F32, name="lift_b")
-            nc.vector.tensor_scalar(lift_b[:], acc[:, 0:LB], base[:, 0:1], None, ALU.add)
+            lift_b = lift_all[:, b, :]
+            nc.vector.tensor_scalar(lift_b, acc[:, 0:LB], base[:, 0:1], None, ALU.add)
             key[b], lift[b] = key_b, lift_b
 
         def build_mask(b):
-            mask_b = sequence.tile([P, PACKED], F32, name="mask_b")
+            mask_b = maskwork.tile([P, PACKED], F32, name="mask_b", tag="step")
             for i in range(LB):
                 nc.vector.scalar_tensor_tensor(
                     block(mask_b, i), block(above, i), valid_sb[:, i, b : b + 1], block(diagonal, i), ALU.mult, ALU.add
@@ -293,27 +318,17 @@ def tile_denoisedsasrec_b_kernel(
                 nc.scalar.copy(res_sb[:], acc[:])
                 nc.sync.dma_start(out[e * P : (e + 1) * P, b * L : (b + 1) * L], res_sb[:])
 
-        first_pair, second_pair = (0, 1), (2, 3)
-        make_first_z()
-        make_vT(0)
-        for b in first_pair:
-            make_key(b)
-        build_shared_mask()
-        for b in first_pair:
-            build_mask(b)
-        make_vT(1)
-        for b in second_pair:
-            make_z(b)
-        for b in first_pair:
-            scores(b)
-        for b in second_pair:
-            make_key(b)
-            build_mask(b)
-        for b in first_pair:
-            mix(b)
-        for b in second_pair:
+        look_up_and_begin_z()
+        for b in range(B):
+            finish_z(b)
+        for b in range(B):
             make_vT(b)
-        for b in second_pair:
+        build_shared_mask()
+        for b in range(B):
+            make_key(b)
+            build_mask(b)
+        scores(0)
+        for b in range(1, B):
             scores(b)
-        for b in second_pair:
-            mix(b)
+            mix(b - 1)
+        mix(B - 1)

@@ -262,7 +262,10 @@ def tile_denoisedsasrec_b_kernel(
                     nc.tensor.matmul(
                         acc[:], fold[:, e, f * P : (f + 1) * P], z[b][:, e, :], start=(e == 0), stop=(e == HB - 1)
                     )
-                nc.vector.tensor_scalar(key_b[:, f, :], acc[:], key_shift[:, f : f + 1], None, ALU.add)
+                if b == 0:
+                    nc.vector.tensor_scalar(key_b[:, f, :], acc[:], key_shift[:, f : f + 1], None, ALU.add)
+                else:
+                    nc.scalar.activation(key_b[:, f, :], acc[:], ACT.Identity, bias=key_shift[:, f : f + 1])
             weighted = None
             for e in range(HB):
                 if e < HB - 1:

@@ -195,7 +195,7 @@ def tile_denoisedsasrec_b_kernel(
                 nc.vector.tensor_mul(crossed(diagonal, i), crossed(above, i), is_diagonal[:])
                 nc.vector.tensor_mul(crossed(above, i), crossed(above, i), is_above[:])
 
-        z, vT, key, lift, mask, p = {}, {}, {}, {}, {}, {}
+        z, vT, weighted, key, lift, mask, p = {}, {}, {}, {}, {}, {}, {}
         lift_all = held.tile([P, B, LB], F32, name="lift_all")
 
         def add_to_z(acc, b, e, c, first, last):
@@ -254,6 +254,22 @@ def tile_denoisedsasrec_b_kernel(
                 nc.scalar.activation(vT_b[:, i, :], acc[:], ACT.Silu)
             vT[b] = vT_b
 
+        def weigh_z(b):
+            partial = None
+            for e in range(HB):
+                if e < HB - 1:
+                    total = summed.tile([P, L], F32, name="partial", tag="x_f32")
+                else:
+                    total = every.tile([P, L], BF16, name="weighted_b")
+                if e == 0:
+                    nc.vector.tensor_scalar(total[:], z[b][:, e, :], lift_weight[:, e : e + 1], None, ALU.mult)
+                else:
+                    nc.vector.scalar_tensor_tensor(
+                        total[:], z[b][:, e, :], lift_weight[:, e : e + 1], partial[:], ALU.mult, ALU.add
+                    )
+                partial = total
+            weighted[b] = partial
+
         def make_key(b):
             key_b = every.tile([P, HB, L], BF16, name="key_b", tag="x")
             for f in range(HB):
@@ -266,22 +282,9 @@ def tile_denoisedsasrec_b_kernel(
                     nc.vector.tensor_scalar(key_b[:, f, :], acc[:], key_shift[:, f : f + 1], None, ALU.add)
                 else:
                     nc.scalar.activation(key_b[:, f, :], acc[:], ACT.Identity, bias=key_shift[:, f : f + 1])
-            weighted = None
-            for e in range(HB):
-                if e < HB - 1:
-                    total = summed.tile([P, L], F32, name="weighted", tag="x_f32")
-                else:
-                    total = sequence.tile([P, L], BF16, name="weighted_sum")
-                if e == 0:
-                    nc.vector.tensor_scalar(total[:], z[b][:, e, :], lift_weight[:, e : e + 1], None, ALU.mult)
-                else:
-                    nc.vector.scalar_tensor_tensor(
-                        total[:], z[b][:, e, :], lift_weight[:, e : e + 1], weighted[:], ALU.mult, ALU.add
-                    )
-                weighted = total
             acc = psum.tile([P, L], F32, name="acc")
             for i in range(LB):
-                nc.tensor.matmul(acc[:, i : i + 1], weighted[:, i * P : (i + 1) * P], ones[:, 0:1], start=True, stop=True)
+                nc.tensor.matmul(acc[:, i : i + 1], weighted[b][:, i * P : (i + 1) * P], ones[:, 0:1], start=True, stop=True)
             lift_b = lift_all[:, b, :]
             nc.vector.tensor_scalar(lift_b, acc[:, 0:LB], base[:, 0:1], None, ALU.add)
             key[b], lift[b] = key_b, lift_b
@@ -325,11 +328,14 @@ def tile_denoisedsasrec_b_kernel(
         for b in range(B):
             finish_z(b)
         for b in range(B):
+            weigh_z(b)
+        for b in range(B):
             make_vT(b)
         build_shared_mask()
         for b in range(B):
-            make_key(b)
             build_mask(b)
+        for b in range(B):
+            make_key(b)
         scores(0)
         for b in range(1, B):
             scores(b)

@@ -196,7 +196,7 @@ def tile_denoisedsasrec_b_kernel(
                 nc.vector.tensor_mul(crossed(above, i), crossed(above, i), is_above[:])
 
         z, vT, weighted, key, lift, mask, p = {}, {}, {}, {}, {}, {}, {}
-        lift_all = held.tile([P, B, LB], F32, name="lift_all")
+        lift_all = held.tile([P, B * LB], F32, name="lift_all")
 
         def add_to_z(acc, b, e, c, first, last):
             nc.tensor.matmul(acc[:], wz_sb[:, c, e::HB], x[b][:, c, :], start=(c == first), stop=(c == last))
@@ -271,23 +271,30 @@ def tile_denoisedsasrec_b_kernel(
             weighted[b] = partial
 
         def make_key(b):
-            key_b = every.tile([P, HB, L], BF16, name="key_b", tag="x")
+            key_b = early.tile([P, HB, L], BF16, name="key_b", tag="early")
             for f in range(HB):
                 acc = psum.tile([P, L], F32, name="acc")
                 for e in range(HB):
                     nc.tensor.matmul(
                         acc[:], fold[:, e, f * P : (f + 1) * P], z[b][:, e, :], start=(e == 0), stop=(e == HB - 1)
                     )
-                if b == 0:
+                if b < 2:
                     nc.vector.tensor_scalar(key_b[:, f, :], acc[:], key_shift[:, f : f + 1], None, ALU.add)
                 else:
                     nc.scalar.activation(key_b[:, f, :], acc[:], ACT.Identity, bias=key_shift[:, f : f + 1])
+            key[b] = key_b
+
+        def make_lift():
             acc = psum.tile([P, L], F32, name="acc")
-            for i in range(LB):
-                nc.tensor.matmul(acc[:, i : i + 1], weighted[b][:, i * P : (i + 1) * P], ones[:, 0:1], start=True, stop=True)
-            lift_b = lift_all[:, b, :]
-            nc.vector.tensor_scalar(lift_b, acc[:, 0:LB], base[:, 0:1], None, ALU.add)
-            key[b], lift[b] = key_b, lift_b
+            for b in range(B):
+                for i in range(LB):
+                    column = b * LB + i
+                    nc.tensor.matmul(
+                        acc[:, column : column + 1], weighted[b][:, i * P : (i + 1) * P], ones[:, 0:1], start=True, stop=True
+                    )
+            nc.vector.tensor_scalar(lift_all[:], acc[:, 0 : B * LB], base[:, 0:1], None, ALU.add)
+            for b in range(B):
+                lift[b] = lift_all[:, b * LB : (b + 1) * LB]
 
         def build_mask(b):
             mask_b = maskwork.tile([P, PACKED], F32, name="mask_b", tag="step")
@@ -327,15 +334,18 @@ def tile_denoisedsasrec_b_kernel(
         look_up_and_begin_z()
         for b in range(B):
             finish_z(b)
+        build_shared_mask()
+        for b in range(2):
+            make_key(b)
         for b in range(B):
             weigh_z(b)
         for b in range(B):
-            make_vT(b)
-        build_shared_mask()
-        for b in range(B):
             build_mask(b)
         for b in range(B):
+            make_vT(b)
+        for b in range(2, B):
             make_key(b)
+        make_lift()
         scores(0)
         for b in range(1, B):
             scores(b)

@@ -56,7 +56,6 @@ def tile_denoisedsasrec_b_kernel(
             return tile
 
         offsets = held.tile([P, N // 16], U16, name="offsets")
-        nc.sync.dma_start(offsets[:], offs)
         table = [held.tile([P, S], F32, name=f"table{c}") for c in range(HB)]
         pos = [held.tile([P, L], F32, name=f"pos{c}") for c in range(HB)]
 
@@ -70,15 +69,17 @@ def tile_denoisedsasrec_b_kernel(
 
         vector_rows = held.tile([FLIPPED_ROWS, P], F32, name="vector_rows")
         nc.gpsimd.memset(vector_rows[:], 0.0)
-        for k, vector in enumerate((gamma_q, beta_q, gamma_k, beta_k)):
-            nc.sync.dma_start(vector_rows[k * HB : (k + 1) * HB, :], vector.rearrange("(d p) o -> d (p o)", p=P))
+
         def load_weight_whole_rows(weight, name):
             tile = early.tile([P, HB, H], BF16, name=name, tag="early")
             nc.sync.dma_start(tile[:], weight.rearrange("(p j) d -> p j d", j=HB))
             return tile
 
         wk_sb = load_weight_whole_rows(wk, "wk_sb")
+        for k, vector in enumerate((gamma_q, beta_q, gamma_k, beta_k)):
+            nc.sync.dma_start(vector_rows[k * HB : (k + 1) * HB, :], vector.rearrange("(d p) o -> d (p o)", p=P))
         wq_sb = load_weight_whole_rows(wq, "wq_sb")
+        nc.sync.dma_start(offsets[:], offs)
         for c in range(HB):
             load_table_block(c)
         wv_sb = load_weight(wv, "wv_sb")
@@ -114,7 +115,10 @@ def tile_denoisedsasrec_b_kernel(
                 bank = psum.tile([P, H], BF16, name="flipped_ps", tag="acc")
                 for e in range(HB):
                     nc.tensor.transpose(bank[:, e * P : (e + 1) * P], weight_sb[:, e, d * P : (d + 1) * P], identity[:])
-                nc.scalar.activation(flipped[:, d, :], bank[:], ACT.Copy, scale=gain[:, d : d + 1])
+                if d % 2 == 0:
+                    nc.scalar.activation(flipped[:, d, :], bank[:], ACT.Copy, scale=gain[:, d : d + 1])
+                else:
+                    nc.vector.tensor_scalar(flipped[:, d, :], bank[:], gain[:, d : d + 1], None, ALU.mult)
             return flipped
 
         fold = held.tile([P, HB, H], BF16, name="fold")

@@ -21,8 +21,9 @@ WIDTH = [L - i * P for i in range(LB)]
 START = [sum(WIDTH[:i]) for i in range(LB)]
 PACKED = sum(WIDTH)
 
+EARLY = 3
 KEPT = 6
-PARKED_PER_BLOCK = 4
+PARKED_AFTER = {1: 6, 2: 6}
 
 
 def block(packed_tile, i):
@@ -47,25 +48,22 @@ def tile_denoisedsasrec_b_kernel(
         tc.tile_pool(name="every", bufs=B) as every,
         tc.tile_pool(name="sequence", bufs=2) as sequence,
         tc.tile_pool(name="maskwork", bufs=4) as maskwork,
-        tc.tile_pool(name="staging", bufs=6) as staging,
+        tc.tile_pool(name="staging", bufs=PARKED_AFTER[1] + PARKED_AFTER[2]) as staging,
         tc.psum_pool(name="psum", bufs=8) as psum,
     ):
-        def load_weight(weight, name):
-            tile = held.tile([P, HB, H], BF16, name=name)
-            nc.sync.dma_start(tile[:], weight.rearrange("(c p) e -> p c e", p=P))
-            return tile
-
         offsets = held.tile([P, N // 16], U16, name="offsets")
         table = [held.tile([P, S], F32, name=f"table{c}") for c in range(HB)]
         pos = [held.tile([P, L], F32, name=f"pos{c}") for c in range(HB)]
 
         wz_sb = held.tile([P, HB, H], BF16, name="wz_sb")
+        wv_sb = held.tile([P, HB, H], BF16, name="wv_sb")
 
         def load_table_block(c):
             rows = slice(c * P, (c + 1) * P)
             nc.sync.dma_start(pos[c][:], pos_emb[rows, :])
             nc.sync.dma_start(table[c][:], item_emb[rows, :])
             nc.sync.dma_start(wz_sb[:, c, :], wz[rows, :])
+            nc.sync.dma_start(wv_sb[:, c, :], wv[rows, :])
 
         vector_rows = held.tile([FLIPPED_ROWS, P], F32, name="vector_rows")
         nc.gpsimd.memset(vector_rows[:], 0.0)
@@ -82,7 +80,6 @@ def tile_denoisedsasrec_b_kernel(
         nc.sync.dma_start(offsets[:], offs)
         for c in range(HB):
             load_table_block(c)
-        wv_sb = load_weight(wv, "wv_sb")
         valid_sb = held.tile([P, LB, B], F32, name="valid_sb")
         nc.sync.dma_start(valid_sb[:], valid.rearrange("(i p) b -> p i b", p=P))
 
@@ -166,11 +163,14 @@ def tile_denoisedsasrec_b_kernel(
 
         x = [every.tile([P, HB, L], BF16, name="x") for b in range(B)]
 
-        def look_up(c, b):
+        def look_up(c, b, rounder):
             x_f32 = summed.tile([P, L], F32, name="x_f32")
             picked = table[c][:].indirect(offsets[:, b * (L // 16) : (b + 1) * (L // 16)])
             nc.vector.tensor_tensor(x_f32[:], picked, pos[c][:], ALU.add)
-            nc.scalar.copy(x[b][:, c, :], x_f32[:])
+            if rounder == "scalar":
+                nc.scalar.copy(x[b][:, c, :], x_f32[:])
+            else:
+                nc.vector.tensor_copy(x[b][:, c, :], x_f32[:])
 
         above = held.tile([P, PACKED], F32, name="above")
         diagonal = held.tile([P, PACKED], F32, name="diagonal")
@@ -202,61 +202,51 @@ def tile_denoisedsasrec_b_kernel(
         z, vT, weighted, key, lift, mask, p = {}, {}, {}, {}, {}, {}, {}
         lift_all = held.tile([P, B * LB], F32, name="lift_all")
 
-        def add_to_z(acc, b, e, c, first, last):
-            nc.tensor.matmul(acc[:], wz_sb[:, c, e::HB], x[b][:, c, :], start=(c == first), stop=(c == last))
+        def add_block(acc, what, b, j, c, first, last):
+            if what == "z":
+                nc.tensor.matmul(acc[:], wz_sb[:, c, j::HB], x[b][:, c, :], start=(c == first), stop=(c == last))
+            else:
+                nc.tensor.matmul(acc[:], x[b][:, c, j * P : (j + 1) * P], wv_sb[:, c, :], start=(c == first), stop=(c == last))
 
-        z_sums = [(b, e) for b in range(B) for e in range(HB)]
+        early_sums = [(what, b, j) for what in ("z", "vT") for b in range(EARLY) for j in range(HB)]
         kept = {}
         parked = {}
 
-        def look_up_and_begin_z():
-            for b, e in z_sums[:KEPT]:
-                kept[(b, e)] = psum.tile([P, L], F32, name="acc")
+        def look_up_and_begin():
+            for name in early_sums[:KEPT]:
+                kept[name] = psum.tile([P, L], F32, name="acc")
+            taken = KEPT
             for c in range(HB):
-                to_park = []
-                if 1 <= c <= HB - 2:
-                    to_park = z_sums[KEPT + (c - 1) * PARKED_PER_BLOCK : KEPT + c * PARKED_PER_BLOCK]
-                urgent = [b for b, e in to_park]
-                for b in sorted(range(B), key=lambda b: b not in urgent):
-                    look_up(c, b)
-                for k, (b, e) in enumerate(to_park):
-                    if k % 2 == 0:
-                        pair = early.tile([P, 2, L], F32, name="pair", tag="early")
+                to_park = early_sums[taken : taken + PARKED_AFTER.get(c, 0)]
+                taken += len(to_park)
+                urgent = [b for what, b, j in to_park]
+                for k, b in enumerate(sorted(range(EARLY), key=lambda b: b not in urgent)):
+                    look_up(c, b, "vector" if k == EARLY - 1 and c < HB - 1 else "scalar")
+                for what, b, j in to_park:
                     acc = psum.tile([P, L], F32, name="acc")
                     for earlier in range(c + 1):
-                        add_to_z(acc, b, e, earlier, 0, c)
-                    nc.scalar.copy(pair[:, k % 2, :], acc[:])
-                    parked[(b, e)] = (pair[:, k % 2, :], c + 1)
-                for b, e in z_sums[:KEPT]:
-                    add_to_z(kept[(b, e)], b, e, c, 0, HB - 1)
+                        add_block(acc, what, b, j, earlier, 0, c)
+                    share = staging.tile([P, L], F32, name="share", tag="res_sb")
+                    nc.scalar.copy(share[:], acc[:])
+                    parked[(what, b, j)] = (share, c + 1)
+                for what, b, j in early_sums[:KEPT]:
+                    add_block(kept[(what, b, j)], what, b, j, c, 0, HB - 1)
 
-        def finish_z(b):
-            z_b = every.tile([P, HB, L], BF16, name="z_b")
-            for e in range(HB):
-                if (b, e) in kept:
-                    whole = kept[(b, e)]
+        def finish(what, b):
+            result = every.tile([P, HB, L], BF16, name="result", tag=what)
+            for j in range(HB):
+                if (what, b, j) in kept:
+                    whole = kept[(what, b, j)]
                 else:
-                    share, begun = parked.get((b, e), (None, 0))
+                    share, begun = parked.get((what, b, j), (None, 0))
                     whole = psum.tile([P, L], F32, name="acc")
                     for c in range(begun, HB):
-                        add_to_z(whole, b, e, c, begun, HB - 1)
+                        add_block(whole, what, b, j, c, begun, HB - 1)
                     if begun > 0:
-                        rest = whole
-                        whole = summed.tile([P, L], F32, name="whole", tag="x_f32")
-                        nc.vector.tensor_tensor(whole[:], rest[:], share, ALU.add)
-                nc.scalar.activation(z_b[:, e, :], whole[:], ACT.Silu)
-            z[b] = z_b
-
-        def make_vT(b):
-            vT_b = every.tile([P, LB, H], BF16, name="vT_b")
-            for i in range(LB):
-                acc = psum.tile([P, H], F32, name="acc")
-                for c in range(HB):
-                    nc.tensor.matmul(
-                        acc[:], x[b][:, c, i * P : (i + 1) * P], wv_sb[:, c, :], start=(c == 0), stop=(c == HB - 1)
-                    )
-                nc.scalar.activation(vT_b[:, i, :], acc[:], ACT.Silu)
-            vT[b] = vT_b
+                        nc.vector.tensor_tensor(share[:], whole[:], share[:], ALU.add)
+                        whole = share
+                nc.scalar.activation(result[:, j, :], whole[:], ACT.Silu)
+            return result
 
         def weigh_z(b):
             partial = None
@@ -335,18 +325,26 @@ def tile_denoisedsasrec_b_kernel(
                 nc.scalar.copy(res_sb[:], acc[:])
                 nc.sync.dma_start(out[e * P : (e + 1) * P, b * L : (b + 1) * L], res_sb[:])
 
-        look_up_and_begin_z()
-        for b in range(B):
-            finish_z(b)
-        build_shared_mask()
+        late = range(EARLY, B)
+        look_up_and_begin()
+        for b in range(EARLY):
+            z[b] = finish("z", b)
         for b in range(2):
             make_key(b)
+            for c in (2 * b, 2 * b + 1):
+                for last in late:
+                    look_up(c, last, "vector")
+        for b in range(EARLY):
+            vT[b] = finish("vT", b)
+        for b in late:
+            z[b] = finish("z", b)
+        build_shared_mask()
         for b in range(B):
             weigh_z(b)
         for b in range(B):
             build_mask(b)
-        for b in range(B):
-            make_vT(b)
+        for b in late:
+            vT[b] = finish("vT", b)
         for b in range(2, B):
             make_key(b)
         make_lift()

@@ -22,8 +22,8 @@ START = [sum(WIDTH[:i]) for i in range(LB)]
 PACKED = sum(WIDTH)
 
 EARLY = 3
-KEPT = 6
-PARKED_AFTER = {1: 6, 2: 6}
+KEPT = 5
+PARKED_AFTER = {1: 7, 2: 6}
 
 
 def block(packed_tile, i):

@@ -272,7 +272,7 @@ def tile_denoisedsasrec_b_kernel(
                     nc.tensor.matmul(
                         acc[:], fold[:, e, f * P : (f + 1) * P], z[b][:, e, :], start=(e == 0), stop=(e == HB - 1)
                     )
-                if b < 2:
+                if b == 0:
                     nc.vector.tensor_scalar(key_b[:, f, :], acc[:], key_shift[:, f : f + 1], None, ALU.add)
                 else:
                     nc.scalar.activation(key_b[:, f, :], acc[:], ACT.Identity, bias=key_shift[:, f : f + 1])

import concourse.mybir as mybir
from concourse.masks import make_identity

F32 = mybir.dt.float32
BF16 = mybir.dt.bfloat16
U16 = mybir.dt.uint16
I32 = mybir.dt.int32
ALU = mybir.AluOpType
ACT = mybir.ActivationFunctionType

P = 128
B, L, H, S = 4, 512, 512, 4096
N = B * L
HB = H // P
LB = L // P
TEMP = 0.2
ROOT = (L * H) ** -0.5
FLIPPED_ROWS = 64

WIDTH = [L - i * P for i in range(LB)]
START = [sum(WIDTH[:i]) for i in range(LB)]
PACKED = sum(WIDTH)

EARLY = 3
KEPT = 5
PARKED_AFTER = {1: 7, 2: 6}


def block(packed_tile, i):
    return packed_tile[:, START[i] : START[i] + WIDTH[i]]


def crossed(packed_tile, i):
    return packed_tile[:, START[i] : START[i] + P]


FLOPS = 4 * 2 * H * H * N + 2 * 2 * H * B * (L * (L + 1) // 2)


def tile_denoisedsasrec_b_kernel(
    tc, item_emb, pos_emb, wz, wv, wq, wk, gamma_q, beta_q, gamma_k, beta_k, sparse_w, gumbel, valid, offs, out
):
    nc = tc.nc
    with (
        tc.tile_pool(name="held", bufs=1) as held,
        tc.tile_pool(name="early", bufs=4) as early,
        tc.tile_pool(name="summed", bufs=4) as summed,
        tc.tile_pool(name="every", bufs=B) as every,
        tc.tile_pool(name="sequence", bufs=2) as sequence,
        tc.tile_pool(name="maskwork", bufs=4) as maskwork,
        tc.tile_pool(name="staging", bufs=PARKED_AFTER[1] + PARKED_AFTER[2]) as staging,
        tc.psum_pool(name="psum", bufs=8) as psum,
    ):
        offsets = held.tile([P, N // 16], U16, name="offsets")
        table = [held.tile([P, S], F32, name=f"table{c}") for c in range(HB)]
        pos = [held.tile([P, L], F32, name=f"pos{c}") for c in range(HB)]

        wz_sb = held.tile([P, HB, H], BF16, name="wz_sb")
        wv_sb = held.tile([P, HB, H], BF16, name="wv_sb")

        def load_table_block(c):
            rows = slice(c * P, (c + 1) * P)
            nc.sync.dma_start(pos[c][:], pos_emb[rows, :])
            nc.sync.dma_start(table[c][:], item_emb[rows, :])
            nc.sync.dma_start(wz_sb[:, c, :], wz[rows, :])
            nc.sync.dma_start(wv_sb[:, c, :], wv[rows, :])

        vector_rows = held.tile([FLIPPED_ROWS, P], F32, name="vector_rows")
        nc.gpsimd.memset(vector_rows[:], 0.0)

        def load_weight_whole_rows(weight, name):
            tile = early.tile([P, HB, H], BF16, name=name, tag="early")
            nc.sync.dma_start(tile[:], weight.rearrange("(p j) d -> p j d", j=HB))
            return tile

        wk_sb = load_weight_whole_rows(wk, "wk_sb")
        for k, vector in enumerate((gamma_q, beta_q, gamma_k, beta_k)):
            nc.sync.dma_start(vector_rows[k * HB : (k + 1) * HB, :], vector.rearrange("(d p) o -> d (p o)", p=P))
        wq_sb = load_weight_whole_rows(wq, "wq_sb")
        nc.sync.dma_start(offsets[:], offs)
        for c in range(HB):
            load_table_block(c)
        valid_sb = held.tile([P, LB, B], F32, name="valid_sb")
        nc.sync.dma_start(valid_sb[:], valid.rearrange("(i p) b -> p i b", p=P))

        warm_up = held.tile([P, 1], F32, name="warm_up")
        nc.gpsimd.memset(warm_up[:], 0.0)
        nc.scalar.activation(warm_up[:], warm_up[:], ACT.Silu)

        identity = held.tile([P, P], BF16, name="identity")
        make_identity(nc, identity[:])
        ones = held.tile([P, P], BF16, name="ones")
        nc.gpsimd.memset(ones[:], 1.0)
        distance = held.tile([P, P], I32, name="distance")
        nc.gpsimd.iota(distance[:], pattern=[[1, P]], base=0, channel_multiplier=-1)
        is_above = held.tile([P, P], F32, name="is_above")
        nc.vector.tensor_scalar(is_above[:], distance[:], 0.0, None, ALU.is_gt)
        is_diagonal = held.tile([P, P], F32, name="is_diagonal")
        nc.vector.tensor_scalar(is_diagonal[:], distance[:], 0.0, None, ALU.is_equal)

        identity_f32 = held.tile([FLIPPED_ROWS, FLIPPED_ROWS], F32, name="identity_f32")
        make_identity(nc, identity_f32[:])
        vector_columns_ps = psum.tile([P, FLIPPED_ROWS], F32, name="vector_columns_ps", tag="acc")
        nc.tensor.transpose(vector_columns_ps[:], vector_rows[:], identity_f32[:])
        vector_columns = held.tile([P, 4 * HB], F32, name="vector_columns")
        nc.vector.tensor_copy(vector_columns[:], vector_columns_ps[:, 0 : 4 * HB])
        gamma_q_sb, beta_q_sb, gamma_k_sb, beta_k_sb = [vector_columns[:, k * HB : (k + 1) * HB] for k in range(4)]

        def flipped_and_gained(weight_sb, gain, name):
            flipped = early.tile([P, HB, H], BF16, name=name, tag="early")
            for d in range(HB):
                bank = psum.tile([P, H], BF16, name="flipped_ps", tag="acc")
                for e in range(HB):
                    nc.tensor.transpose(bank[:, e * P : (e + 1) * P], weight_sb[:, e, d * P : (d + 1) * P], identity[:])
                if d % 2 == 0:
                    nc.scalar.activation(flipped[:, d, :], bank[:], ACT.Copy, scale=gain[:, d : d + 1])
                else:
                    nc.vector.tensor_scalar(flipped[:, d, :], bank[:], gain[:, d : d + 1], None, ALU.mult)
            return flipped

        fold = held.tile([P, HB, H], BF16, name="fold")
        key_shift = held.tile([P, HB], F32, name="key_shift")
        lift_weight = held.tile([P, HB], F32, name="lift_weight")
        base = held.tile([P, 1], F32, name="base")

        def fold_weights():
            gamma_k_rooted = held.tile([P, HB], F32, name="gamma_k_rooted")
            nc.vector.tensor_scalar(gamma_k_rooted[:], gamma_k_sb, ROOT, None, ALU.mult)
            wkT = flipped_and_gained(wk_sb, gamma_k_rooted, "wkT")
            wqT = flipped_and_gained(wq_sb, gamma_q_sb, "wqT")
            for e in range(HB):
                acc = psum.tile([P, H], F32, name="acc")
                for d in range(HB):
                    nc.tensor.matmul(acc[:], wkT[:, d, e * P : (e + 1) * P], wqT[:, d, :], start=(d == 0), stop=(d == HB - 1))
                nc.scalar.copy(fold[:, e, :], acc[:])

            shift_q = held.tile([P, HB], BF16, name="shift_q")
            nc.vector.tensor_copy(shift_q[:], beta_q_sb)
            shift_k_rooted = held.tile([P, HB], BF16, name="shift_k_rooted")
            nc.vector.tensor_scalar(shift_k_rooted[:], beta_k_sb, ROOT, None, ALU.mult)
            shifts_rooted = held.tile([P, HB], BF16, name="shifts_rooted")
            nc.vector.scalar_tensor_tensor(shifts_rooted[:], beta_k_sb, ROOT, beta_q_sb, ALU.mult, ALU.mult)
            acc = psum.tile([P, H], F32, name="acc")
            for flipped, vector, first in ((wkT, shift_q, 0), (wqT, shift_k_rooted, HB)):
                for e in range(HB):
                    for d in range(HB):
                        nc.tensor.matmul(
                            acc[:, first + e : first + e + 1],
                            flipped[:, d, e * P : (e + 1) * P],
                            vector[:, d : d + 1],
                            start=(d == 0),
                            stop=(d == HB - 1),
                        )
            for d in range(HB):
                nc.tensor.matmul(
                    acc[:, 2 * HB : 2 * HB + 1], ones[:], shifts_rooted[:, d : d + 1], start=(d == 0), stop=(d == HB - 1)
                )
            nc.scalar.copy(lift_weight[:], acc[:, 0:HB])
            nc.scalar.copy(key_shift[:], acc[:, HB : 2 * HB])
            nc.scalar.copy(base[:], acc[:, 2 * HB : 2 * HB + 1])

        fold_weights()

        x = [every.tile([P, HB, L], BF16, name="x") for b in range(B)]

        def look_up(c, b, rounder):
            x_f32 = summed.tile([P, L], F32, name="x_f32")
            picked = table[c][:].indirect(offsets[:, b * (L // 16) : (b + 1) * (L // 16)])
            nc.vector.tensor_tensor(x_f32[:], picked, pos[c][:], ALU.add)
            if rounder == "scalar":
                nc.scalar.copy(x[b][:, c, :], x_f32[:])
            else:
                nc.vector.tensor_copy(x[b][:, c, :], x_f32[:])

        above = held.tile([P, PACKED], F32, name="above")
        diagonal = held.tile([P, PACKED], F32, name="diagonal")
        nc.gpsimd.memset(diagonal[:], 0.0)

        def build_shared_mask():
            def step(name):
                return maskwork.tile([P, PACKED], F32, name=name, tag="step")

            w_sb = step("w_sb")
            g_sb = step("g_sb")
            for i in range(LB):
                rows = slice(i * P, (i + 1) * P)
                nc.sync.dma_start(block(w_sb, i), sparse_w[rows, i * P : L])
                nc.sync.dma_start(block(g_sb, i), gumbel[rows, i * P : L])
            ln_w = step("ln_w")
            nc.scalar.activation(ln_w[:], w_sb[:], ACT.Ln)
            ln_rest = step("ln_rest")
            nc.scalar.activation(ln_rest[:], w_sb[:], ACT.Ln, bias=1.0, scale=-1.0)
            noisy = step("noisy")
            nc.vector.tensor_add(noisy[:], ln_w[:], g_sb[:])
            logit = step("logit")
            nc.vector.tensor_sub(logit[:], noisy[:], ln_rest[:])
            nc.scalar.activation(above[:], logit[:], ACT.Sigmoid, scale=1.0 / TEMP)
            for i in range(LB):
                nc.vector.tensor_mul(crossed(diagonal, i), crossed(above, i), is_diagonal[:])
                nc.vector.tensor_mul(crossed(above, i), crossed(above, i), is_above[:])

        z, vT, weighted, key, lift, mask, p = {}, {}, {}, {}, {}, {}, {}
        lift_all = held.tile([P, B * LB], F32, name="lift_all")

        def add_block(acc, what, b, j, c, first, last):
            if what == "z":
                nc.tensor.matmul(acc[:], wz_sb[:, c, j::HB], x[b][:, c, :], start=(c == first), stop=(c == last))
            else:
                nc.tensor.matmul(acc[:], x[b][:, c, j * P : (j + 1) * P], wv_sb[:, c, :], start=(c == first), stop=(c == last))

        early_sums = [(what, b, j) for what in ("z", "vT") for b in range(EARLY) for j in range(HB)]
        kept = {}
        parked = {}

        def look_up_and_begin():
            for name in early_sums[:KEPT]:
                kept[name] = psum.tile([P, L], F32, name="acc")
            taken = KEPT
            for c in range(HB):
                to_park = early_sums[taken : taken + PARKED_AFTER.get(c, 0)]
                taken += len(to_park)
                urgent = [b for what, b, j in to_park]
                for k, b in enumerate(sorted(range(EARLY), key=lambda b: b not in urgent)):
                    look_up(c, b, "vector" if k == EARLY - 1 and c < HB - 1 else "scalar")
                for what, b, j in to_park:
                    acc = psum.tile([P, L], F32, name="acc")
                    for earlier in range(c + 1):
                        add_block(acc, what, b, j, earlier, 0, c)
                    share = staging.tile([P, L], F32, name="share", tag="res_sb")
                    nc.scalar.copy(share[:], acc[:])
                    parked[(what, b, j)] = (share, c + 1)
                for what, b, j in early_sums[:KEPT]:
                    add_block(kept[(what, b, j)], what, b, j, c, 0, HB - 1)

        def finish(what, b):
            result = every.tile([P, HB, L], BF16, name="result", tag=what)
            for j in range(HB):
                if (what, b, j) in kept:
                    whole = kept[(what, b, j)]
                else:
                    share, begun = parked.get((what, b, j), (None, 0))
                    whole = psum.tile([P, L], F32, name="acc")
                    for c in range(begun, HB):
                        add_block(whole, what, b, j, c, begun, HB - 1)
                    if begun > 0:
                        nc.vector.tensor_tensor(share[:], whole[:], share[:], ALU.add)
                        whole = share
                nc.scalar.activation(result[:, j, :], whole[:], ACT.Silu)
            return result

        def weigh_z(b):
            partial = None
            for e in range(HB):
                if e < HB - 1:
                    total = summed.tile([P, L], F32, name="partial", tag="x_f32")
                else:
                    total = every.tile([P, L], BF16, name="weighted_b")
                if e == 0:
                    nc.vector.tensor_scalar(total[:], z[b][:, e, :], lift_weight[:, e : e + 1], None, ALU.mult)
                else:
                    nc.vector.scalar_tensor_tensor(
                        total[:], z[b][:, e, :], lift_weight[:, e : e + 1], partial[:], ALU.mult, ALU.add
                    )
                partial = total
            weighted[b] = partial

        def make_key(b):
            key_b = early.tile([P, HB, L], BF16, name="key_b", tag="early")
            for f in range(HB):
                acc = psum.tile([P, L], F32, name="acc")
                for e in range(HB):
                    nc.tensor.matmul(
                        acc[:], fold[:, e, f * P : (f + 1) * P], z[b][:, e, :], start=(e == 0), stop=(e == HB - 1)
                    )
                if b == 0:
                    nc.vector.tensor_scalar(key_b[:, f, :], acc[:], key_shift[:, f : f + 1], None, ALU.add)
                else:
                    nc.scalar.activation(key_b[:, f, :], acc[:], ACT.Identity, bias=key_shift[:, f : f + 1])
            key[b] = key_b

        def make_lift():
            acc = psum.tile([P, L], F32, name="acc")
            for b in range(B):
                for i in range(LB):
                    column = b * LB + i
                    nc.tensor.matmul(
                        acc[:, column : column + 1], weighted[b][:, i * P : (i + 1) * P], ones[:, 0:1], start=True, stop=True
                    )
            nc.vector.tensor_scalar(lift_all[:], acc[:, 0 : B * LB], base[:, 0:1], None, ALU.add)
            for b in range(B):
                lift[b] = lift_all[:, b * LB : (b + 1) * LB]

        def build_mask(b):
            mask_b = maskwork.tile([P, PACKED], F32, name="mask_b", tag="step")
            for i in range(LB):
                nc.vector.scalar_tensor_tensor(
                    block(mask_b, i), block(above, i), valid_sb[:, i, b : b + 1], block(diagonal, i), ALU.mult, ALU.add
                )
            mask[b] = mask_b

        def scores(b):
            masked = sequence.tile([P, PACKED], F32, name="masked")
            for i in range(LB):
                cols = slice(i * P, L)
                acc = psum.tile([P, L], F32, name="acc")
                for f in range(HB):
                    nc.tensor.matmul(
                        acc[:, cols], key[b][:, f, i * P : (i + 1) * P], z[b][:, f, cols], start=(f == 0), stop=(f == HB - 1)
                    )
                nc.vector.scalar_tensor_tensor(
                    block(masked, i), acc[:, cols], lift[b][:, i : i + 1], block(mask[b], i), ALU.add, ALU.mult
                )
            p_b = sequence.tile([P, PACKED], BF16, name="p_b")
            nc.vector.scalar_tensor_tensor(p_b[:], masked[:], 0.0, masked[:], ALU.max, ALU.mult)
            p[b] = p_b

        def mix(b):
            for e in range(HB):
                acc = psum.tile([P, L], F32, name="acc")
                for i in range(LB):
                    nc.tensor.matmul(
                        acc[:, i * P : L], vT[b][:, i, e * P : (e + 1) * P], block(p[b], i), start=(i == 0), stop=(i == LB - 1)
                    )
                res_sb = staging.tile([P, L], F32, name="res_sb")
                nc.scalar.copy(res_sb[:], acc[:])
                nc.sync.dma_start(out[e * P : (e + 1) * P, b * L : (b + 1) * L], res_sb[:])

        late = range(EARLY, B)
        look_up_and_begin()
        for b in range(EARLY):
            z[b] = finish("z", b)
        for b in range(2):
            make_key(b)
            for c in (2 * b, 2 * b + 1):
                for last in late:
                    look_up(c, last, "vector")
        for b in range(EARLY):
            vT[b] = finish("vT", b)
        for b in late:
            z[b] = finish("z", b)
        build_shared_mask()
        for b in range(B):
            weigh_z(b)
        for b in range(B):
            build_mask(b)
        for b in late:
            vT[b] = finish("vT", b)
        for b in range(2, B):
            make_key(b)
        make_lift()
        scores(0)
        for b in range(1, B):
            scores(b)
            mix(b - 1)
        mix(B - 1)
